import numpy as np
import ml_dtypes


def mxq(x, axis, fmt="e4m3"):
    dtype, down = {"e4m3": (ml_dtypes.float8_e4m3fn, 7), "e5m2": (ml_dtypes.float8_e5m2, 14)}[fmt]
    v = np.moveaxis(np.asarray(x, np.float32).astype(ml_dtypes.bfloat16).astype(np.float64), axis, -1)
    blocks = v.reshape(v.shape[:-1] + (-1, 32))
    amax = np.abs(blocks).max(-1, keepdims=True)
    byte = np.maximum(np.where(amax > 0, np.frexp(amax)[1] - 1 + 127, 0) - down, 1)
    scale = np.exp2(byte - 127.0)
    codes = (blocks / scale).astype(np.float32).astype(dtype).astype(np.float64)
    return np.moveaxis((codes * scale).reshape(v.shape), -1, axis)


WIDE = False


def mx_kscale(k):
    if not WIDE:
        return np.ones(k)
    levels = np.array([10, -10, 5, -5, 0])
    a = np.random.permutation(np.resize(levels, k // 512 * 4)).reshape(k // 512, 4)
    idx = np.arange(k)
    return np.exp2(a[idx // 512, idx % 128 // 32])


BF16 = ml_dtypes.bfloat16


def bf(x):
    return np.asarray(x, np.float32).astype(BF16)


def f64(x):
    return np.asarray(x).astype(np.float64)


B, N, D, H, DH = 4, 1024, 512, 1, 128
E = H * DH
K_POLY = 3
SIG = 2.0


def setup_inputs():
    s = mx_kscale(D)
    g = np.random.standard_normal
    lg = g((B, H, N, N)) * SIG
    e = np.exp(lg - lg.max(-1, keepdims=True))
    return {
        "x": bf(g((B, N, D)) * s),
        "att": bf(e / e.sum(-1, keepdims=True)),
        "Wv": bf(g((D, E)) * 1.5 / np.sqrt(D) / s[:, None]),
        "bv": bf(g(E) * 0.2),
        "w0": bf(0.25 + 0.05 * g(H)),
        "w1": bf(1.0 + 0.1 * g(H)),
        "wK": bf(0.2 + 0.03 * g(H)),
    }


def reference(x, att, Wv, bv, w0, w1, wK):
    v = (mxq(f64(x), 2, "e4m3") @ mxq(f64(Wv), 0, "e4m3")) + f64(bv)
    v = v.reshape(B, N, H, DH).transpose(0, 2, 1, 3)
    att = f64(att)
    att2 = mxq(att, 3, "e4m3") @ mxq(att, 2, "e4m3")
    attK = att + (K_POLY - 1) * (att2 - att)
    c0 = f64(w0)[None, :, None, None]
    c1 = f64(w1)[None, :, None, None]
    cK = f64(wK)[None, :, None, None]
    gf = c0 * np.eye(N)[None, None] + c1 * att + cK * attK
    out = mxq(gf, 3, "e4m3") @ mxq(v, 2, "e4m3")
    return out.transpose(0, 2, 1, 3).reshape(B, N, E)

@@ -1,0 +1,268 @@
+from contextlib import ExitStack
+
+import concourse.mybir as mybir
+from concourse.masks import make_identity
+
+F32 = mybir.dt.float32
+BF16 = mybir.dt.bfloat16
+U32 = mybir.dt.uint32
+U8 = mybir.dt.uint8
+FP8X4 = mybir.dt.float8_e4m3fn_x4
+ALU = mybir.AluOpType
+ACT = mybir.ActivationFunctionType
+
+B, N, D, DH = 4, 1024, 512, 128
+P = 128
+PACK = 4
+HALF = 512
+ROW_TILES = N // P
+UNITS = 4
+LAG = 3
+
+FLOPS = 2 * B * (N * D * DH + N * N * N + N * N * DH)
+
+
+def tile_gfsa_pa_t_kernel(tc, x, att, Wv, bv, w0, w1, wK, out):
+    nc = tc.nc
+    with ExitStack() as ctx:
+        const = ctx.enter_context(tc.tile_pool(name="const", bufs=1))
+        per_batch = ctx.enter_context(tc.tile_pool(name="per_batch", bufs=2))
+        per_unit = ctx.enter_context(tc.tile_pool(name="per_unit", bufs=3))
+        psum_turn = ctx.enter_context(tc.psum_pool(name="psum_turn", bufs=3))
+        psum_att2 = ctx.enter_context(tc.psum_pool(name="psum_att2", bufs=3))
+        psum_small = ctx.enter_context(tc.psum_pool(name="psum_small", bufs=2))
+
+        def quantise(codes, scales, grouped):
+            nc.vector.quantize_mx(out=codes.bitcast(FP8X4), scales=scales, in_=grouped)
+
+        def mx(acc, left, right, start, stop):
+            nc.tensor.matmul_mx(
+                out=acc,
+                lhsT=left[0].bitcast(FP8X4),
+                lhsT_scale=left[1],
+                rhs=right[0].bitcast(FP8X4),
+                rhs_scale=right[1],
+                start=start,
+                stop=stop,
+            )
+
+        def load_batch(b):
+            a_rows = per_batch.tile([P, ROW_TILES, N], BF16, name="a_rows")
+            x_rows = per_batch.tile([P, ROW_TILES, D], BF16, name="x_rows")
+            a_chunks = att[b, 0].rearrange("(c p e) m -> c p e m", p=P, e=2)
+            x_chunks = x[b].rearrange("(c p e) d -> c p e d", p=P, e=2)
+            for c in range(ROW_TILES // 2):
+                nc.sync.dma_start(out=a_rows[:, 2 * c : 2 * c + 2, :], in_=a_chunks[c])
+                nc.sync.dma_start(out=x_rows[:, 2 * c : 2 * c + 2, :], in_=x_chunks[c])
+            return a_rows, x_rows
+
+        rows = {0: load_batch(0)}
+
+        ident = const.tile([P, P], F32)
+        make_identity(nc, ident[:])
+
+        w0_bf = const.tile([P, 1], BF16)
+        w1_bf = const.tile([P, 1], BF16)
+        wk_bf = const.tile([P, 1], BF16)
+        bias = const.tile([P, DH], BF16)
+        wv_rows = const.tile([P, PACK, DH], BF16)
+        nc.scalar.dma_start(out=w0_bf[:], in_=w0.partition_broadcast(P))
+        nc.scalar.dma_start(out=w1_bf[:], in_=w1.partition_broadcast(P))
+        nc.scalar.dma_start(out=wk_bf[:], in_=wK.partition_broadcast(P))
+        nc.scalar.dma_start(out=bias[:], in_=bv.partition_broadcast(P))
+        nc.scalar.dma_start(
+            out=wv_rows[:].rearrange("p (u e) n -> p u e n", e=2),
+            in_=Wv.rearrange("(u p e) n -> p u e n", p=P, e=2),
+        )
+
+        lin = const.tile([P, 1], F32)
+        quad = const.tile([P, 1], F32)
+        w0_f32 = const.tile([P, 1], F32)
+        w0_ident = const.tile([P, P], F32)
+        nc.vector.tensor_tensor(out=lin[:], in0=w1_bf[:], in1=wk_bf[:], op=ALU.subtract)
+        nc.vector.tensor_scalar(out=quad[:], in0=wk_bf[:], scalar1=2.0, scalar2=None, op0=ALU.mult)
+        nc.vector.tensor_copy(out=w0_f32[:], in_=w0_bf[:])
+        nc.vector.tensor_scalar(
+            out=w0_ident[:], in0=ident[:], scalar1=w0_f32[:, 0:1], scalar2=None, op0=ALU.mult
+        )
+
+        wv_grouped = const.tile([P, DH, PACK], BF16, align_bytes=64)
+        wv_codes = const.tile([P, DH], U32, align_bytes=64)
+        wv_scales = const.tile([P, DH], U8, align_bytes=64)
+        nc.vector.tensor_copy(out=wv_grouped[:], in_=wv_rows[:].rearrange("p t n -> p n t"))
+        quantise(wv_codes[:], wv_scales[:], wv_grouped[:].rearrange("p n t -> p (n t)"))
+
+        def batch_tiles():
+            a_codes = per_batch.tile([P, 2, N], U32, align_bytes=64, name="a_codes")
+            a_scales = per_batch.tile([P, 2, N], U8, align_bytes=64, name="a_scales")
+            at_grouped = per_batch.tile([P, 2, N, PACK], BF16, align_bytes=64, name="at_grouped")
+            at_codes = per_batch.tile([P, 2, N], U32, align_bytes=64, name="at_codes")
+            at_scales = per_batch.tile([P, 2, N], U8, align_bytes=64, name="at_scales")
+            x_codes = per_batch.tile([P, N], U32, align_bytes=64, name="x_codes")
+            x_scales = per_batch.tile([P, N], U8, align_bytes=64, name="x_scales")
+            v_codes = per_batch.tile([P, 2, DH], U32, align_bytes=64, name="v_codes")
+            v_scales = per_batch.tile([P, 2, DH], U8, align_bytes=64, name="v_scales")
+            gf_codes = per_batch.tile([P, 2, N], U32, align_bytes=64, name="gf_codes")
+            gf_scales = per_batch.tile([P, 2, N], U8, align_bytes=64, name="gf_scales")
+            return {
+                "a": (a_codes, a_scales),
+                "at_grouped": at_grouped,
+                "at": (at_codes, at_scales),
+                "x": (x_codes, x_scales),
+                "v": (v_codes, v_scales),
+                "gf": (gf_codes, gf_scales),
+            }
+
+        def turn(bank, words, row_tile, first_word):
+            for u in range(2):
+                for i in range(2):
+                    nc.tensor.transpose(
+                        bank[:, u, i * P : (i + 1) * P],
+                        words[:, row_tile + i, first_word + u * P : first_word + (u + 1) * P],
+                        ident[:],
+                    )
+
+        def prepare(b, j, t):
+            a_rows, x_rows = rows[b]
+            side, g = j // 2, j % 2
+            cols = slice(side * HALF, (side + 1) * HALF)
+
+            at_words = t["at_grouped"][:].bitcast(F32)
+            for pair in range(2 * side, 2 * side + 2):
+                bank = psum_turn.tile([P, 2, 2 * P], F32, name="bank")
+                turn(bank, a_rows[:].bitcast(F32), 2 * pair, g * (HALF // 2))
+                nc.scalar.copy(
+                    out=at_words[:, g, pair * 2 * P : (pair + 1) * 2 * P, :],
+                    in_=bank[:].rearrange("p u n -> p n u"),
+                )
+
+            a_grouped = per_unit.tile([P, HALF, PACK], BF16, align_bytes=64, name="a_grouped")
+
+            def key_block(i):
+                c = 2 * side + i
+                grouped = a_grouped[:, i * 2 * P : (i + 1) * 2 * P, :]
+                lying = a_rows[:, PACK * g : PACK * (g + 1), c * 2 * P : (c + 1) * 2 * P]
+                return (
+                    grouped.rearrange("p (e q) t -> p e q t", e=2),
+                    lying.rearrange("p t (q e) -> p e q t", e=2),
+                )
+
+            grouped, lying = key_block(0)
+            nc.vector.tensor_copy(out=grouped, in_=lying)
+            grouped, lying = key_block(1)
+            nc.scalar.copy(out=grouped, in_=lying)
+
+            bank = psum_turn.tile([P, 2, 2 * P], F32, name="bank")
+            turn(bank, x_rows[:].bitcast(F32), 2 * j, 0)
+            xt_grouped = per_unit.tile([P, 2 * P, PACK], BF16, align_bytes=64, name="xt_grouped")
+            nc.scalar.copy(out=xt_grouped[:].bitcast(F32), in_=bank[:].rearrange("p u n -> p n u"))
+
+            quantise(
+                t["at"][0][:, g, cols],
+                t["at"][1][:, g, cols],
+                t["at_grouped"][:, g, cols, :].rearrange("p n t -> p (n t)"),
+            )
+            quantise(
+                t["a"][0][:, g, cols],
+                t["a"][1][:, g, cols],
+                a_grouped[:].rearrange("p m t -> p (m t)"),
+            )
+            tokens = slice(j * 2 * P, (j + 1) * 2 * P)
+            quantise(
+                t["x"][0][:, tokens],
+                t["x"][1][:, tokens],
+                xt_grouped[:].rearrange("p n t -> p (n t)"),
+            )
+
+            if j % 2 == 1:
+                pas = j // 2
+                v_bank = psum_small.tile([P, PACK, DH], F32, name="small_bank")
+                for k in range(PACK):
+                    tile_cols = slice((PACK * pas + k) * P, (PACK * pas + k + 1) * P)
+                    mx(
+                        v_bank[:, k, :],
+                        (t["x"][0][:, tile_cols], t["x"][1][:, tile_cols]),
+                        (wv_codes[:], wv_scales[:]),
+                        True,
+                        True,
+                    )
+                v_grouped = per_unit.tile([P, DH, PACK], BF16, align_bytes=64, name="v_grouped")
+                nc.vector.tensor_tensor(
+                    out=v_grouped[:],
+                    in0=v_bank[:].rearrange("p t d -> p d t"),
+                    in1=bias[:].unsqueeze(2).to_broadcast([P, DH, PACK]),
+                    op=ALU.add,
+                )
+                quantise(
+                    t["v"][0][:, pas, :],
+                    t["v"][1][:, pas, :],
+                    v_grouped[:].rearrange("p d t -> p (d t)"),
+                )
+
+        def finish(b, i, t):
+            side, pas = i // 2, i % 2
+            cols = slice(side * HALF, (side + 1) * HALF)
+
+            scaled = per_unit.tile([P, PACK, HALF], F32, name="scaled")
+            for k in range(PACK):
+                key_cols = slice((PACK * pas + k) * P, (PACK * pas + k + 1) * P)
+                acc = psum_att2.tile([P, HALF], F32, name="acc")
+                for g in range(2):
+                    mx(
+                        acc[:],
+                        (t["a"][0][:, g, key_cols], t["a"][1][:, g, key_cols]),
+                        (t["at"][0][:, g, cols], t["at"][1][:, g, cols]),
+                        g == 0,
+                        g == 1,
+                    )
+                nc.scalar.activation(out=scaled[:, k, :], in_=acc[:], func=ACT.Copy, scale=quad[:, 0:1])
+                if side == pas:
+                    block = scaled[:, k, k * P : (k + 1) * P]
+                    nc.vector.tensor_tensor(out=block, in0=block, in1=w0_ident[:], op=ALU.add)
+
+            gf_grouped = per_unit.tile([P, HALF, PACK], BF16, align_bytes=64, name="gf_grouped")
+            nc.vector.scalar_tensor_tensor(
+                out=gf_grouped[:],
+                in0=t["at_grouped"][:, pas, cols, :],
+                scalar=lin[:, 0:1],
+                in1=scaled[:].rearrange("p t n -> p n t"),
+                op0=ALU.mult,
+                op1=ALU.add,
+            )
+            quantise(
+                t["gf"][0][:, pas, cols],
+                t["gf"][1][:, pas, cols],
+                gf_grouped[:].rearrange("p n t -> p (n t)"),
+            )
+
+            if pas == 1:
+                o_bank = psum_small.tile([P, PACK, DH], F32, name="small_bank")
+                for k in range(PACK):
+                    query_cols = slice((PACK * side + k) * P, (PACK * side + k + 1) * P)
+                    for g in range(2):
+                        mx(
+                            o_bank[:, k, :],
+                            (t["gf"][0][:, g, query_cols], t["gf"][1][:, g, query_cols]),
+                            (t["v"][0][:, g, :], t["v"][1][:, g, :]),
+                            g == 0,
+                            g == 1,
+                        )
+                o_rows = per_unit.tile([P, PACK, DH], F32, name="o_rows")
+                nc.scalar.copy(out=o_rows[:], in_=o_bank[:])
+                nc.sync.dma_start(
+                    out=out[b, cols, :].rearrange("(u p e) d -> p u e d", p=P, e=2),
+                    in_=o_rows[:].rearrange("p (u e) d -> p u e d", e=2),
+                )
+
+        tiles = {}
+        for step in range(B * UNITS + LAG):
+            if step < B * UNITS:
+                b, j = divmod(step, UNITS)
+                if j == 0:
+                    tiles[b] = batch_tiles()
+                    if b + 1 < B:
+                        rows[b + 1] = load_batch(b + 1)
+                prepare(b, j, tiles[b])
+            if step >= LAG:
+                b, i = divmod(step - LAG, UNITS)
+                finish(b, i, tiles[b])

@@ -16,8 +16,13 @@ P = 128
 PACK = 4
 HALF = 512
 ROW_TILES = N // P
-UNITS = 4
-LAG = 3
+UNITS = 4 * B
+
+QUANTISE_LAG = 1
+VALUES_LAG = 2
+ATT2_LAG = 4
+COMBINE_LAG = 5
+OUT_LAG = 7
 
 FLOPS = 2 * B * (N * D * DH + N * N * N + N * N * DH)
 
@@ -26,14 +31,22 @@ def tile_gfsa_pa_t_kernel(tc, x, att, Wv, bv, w0, w1, wK, out):
     nc = tc.nc
     with ExitStack() as ctx:
         const = ctx.enter_context(tc.tile_pool(name="const", bufs=1))
-        per_batch = ctx.enter_context(tc.tile_pool(name="per_batch", bufs=2))
-        per_unit = ctx.enter_context(tc.tile_pool(name="per_unit", bufs=3))
+        sbuf = ctx.enter_context(tc.tile_pool(name="sbuf", bufs=3))
         psum_turn = ctx.enter_context(tc.psum_pool(name="psum_turn", bufs=3))
         psum_att2 = ctx.enter_context(tc.psum_pool(name="psum_att2", bufs=3))
         psum_small = ctx.enter_context(tc.psum_pool(name="psum_small", bufs=2))
+        ctx.enter_context(tc.manual_schedule())
 
-        def quantise(codes, scales, grouped):
-            nc.vector.quantize_mx(out=codes.bitcast(FP8X4), scales=scales, in_=grouped)
+        def operand(name, columns, bufs):
+            codes = sbuf.tile([P, columns], U32, align_bytes=64, name=name + "_codes", bufs=bufs)
+            scales = sbuf.tile([P, columns], U8, align_bytes=64, name=name + "_scales", bufs=bufs)
+            return codes, scales
+
+        def columns_of(pair, first, count):
+            return pair[0][:, first : first + count], pair[1][:, first : first + count]
+
+        def quantise(pair, grouped):
+            nc.vector.quantize_mx(out=pair[0][:].bitcast(FP8X4), scales=pair[1][:], in_=grouped)
 
         def mx(acc, left, right, start, stop):
             nc.tensor.matmul_mx(
@@ -46,17 +59,21 @@ def tile_gfsa_pa_t_kernel(tc, x, att, Wv, bv, w0, w1, wK, out):
                 stop=stop,
             )
 
+        a_rows, x_rows = {}, {}
+        turn_banks, at_grouped, a_grouped, xt_grouped = {}, {}, {}, {}
+        at_q, a_q, x_q, v_q, gf_q = {}, {}, {}, {}, {}
+        v_banks, v_grouped, scaled, gf_grouped = {}, {}, {}, {}
+
         def load_batch(b):
-            a_rows = per_batch.tile([P, ROW_TILES, N], BF16, name="a_rows")
-            x_rows = per_batch.tile([P, ROW_TILES, D], BF16, name="x_rows")
+            a_rows[b] = sbuf.tile([P, ROW_TILES, N], BF16, name="a_rows", bufs=2)
+            x_rows[b] = sbuf.tile([P, ROW_TILES, D], BF16, name="x_rows", bufs=2)
             a_chunks = att[b, 0].rearrange("(c p e) m -> c p e m", p=P, e=2)
             x_chunks = x[b].rearrange("(c p e) d -> c p e d", p=P, e=2)
             for c in range(ROW_TILES // 2):
-                nc.sync.dma_start(out=a_rows[:, 2 * c : 2 * c + 2, :], in_=a_chunks[c])
-                nc.sync.dma_start(out=x_rows[:, 2 * c : 2 * c + 2, :], in_=x_chunks[c])
-            return a_rows, x_rows
+                nc.sync.dma_start(out=a_rows[b][:, 2 * c : 2 * c + 2, :], in_=a_chunks[c])
+                nc.sync.dma_start(out=x_rows[b][:, 2 * c : 2 * c + 2, :], in_=x_chunks[c])
 
-        rows = {0: load_batch(0)}
+        load_batch(0)
 
         ident = const.tile([P, P], F32)
         make_identity(nc, ident[:])
@@ -79,41 +96,24 @@ def tile_gfsa_pa_t_kernel(tc, x, att, Wv, bv, w0, w1, wK, out):
         quad = const.tile([P, 1], F32)
         w0_f32 = const.tile([P, 1], F32)
         w0_ident = const.tile([P, P], F32)
-        nc.vector.tensor_tensor(out=lin[:], in0=w1_bf[:], in1=wk_bf[:], op=ALU.subtract)
-        nc.vector.tensor_scalar(out=quad[:], in0=wk_bf[:], scalar1=2.0, scalar2=None, op0=ALU.mult)
-        nc.vector.tensor_copy(out=w0_f32[:], in_=w0_bf[:])
-        nc.vector.tensor_scalar(
-            out=w0_ident[:], in0=ident[:], scalar1=w0_f32[:, 0:1], scalar2=None, op0=ALU.mult
-        )
-
         wv_grouped = const.tile([P, DH, PACK], BF16, align_bytes=64)
         wv_codes = const.tile([P, DH], U32, align_bytes=64)
         wv_scales = const.tile([P, DH], U8, align_bytes=64)
-        nc.vector.tensor_copy(out=wv_grouped[:], in_=wv_rows[:].rearrange("p t n -> p n t"))
-        quantise(wv_codes[:], wv_scales[:], wv_grouped[:].rearrange("p n t -> p (n t)"))
 
-        def batch_tiles():
-            a_codes = per_batch.tile([P, 2, N], U32, align_bytes=64, name="a_codes")
-            a_scales = per_batch.tile([P, 2, N], U8, align_bytes=64, name="a_scales")
-            at_grouped = per_batch.tile([P, 2, N, PACK], BF16, align_bytes=64, name="at_grouped")
-            at_codes = per_batch.tile([P, 2, N], U32, align_bytes=64, name="at_codes")
-            at_scales = per_batch.tile([P, 2, N], U8, align_bytes=64, name="at_scales")
-            x_codes = per_batch.tile([P, N], U32, align_bytes=64, name="x_codes")
-            x_scales = per_batch.tile([P, N], U8, align_bytes=64, name="x_scales")
-            v_codes = per_batch.tile([P, 2, DH], U32, align_bytes=64, name="v_codes")
-            v_scales = per_batch.tile([P, 2, DH], U8, align_bytes=64, name="v_scales")
-            gf_codes = per_batch.tile([P, 2, N], U32, align_bytes=64, name="gf_codes")
-            gf_scales = per_batch.tile([P, 2, N], U8, align_bytes=64, name="gf_scales")
-            return {
-                "a": (a_codes, a_scales),
-                "at_grouped": at_grouped,
-                "at": (at_codes, at_scales),
-                "x": (x_codes, x_scales),
-                "v": (v_codes, v_scales),
-                "gf": (gf_codes, gf_scales),
-            }
+        def prepare_constants():
+            nc.vector.tensor_copy(out=wv_grouped[:], in_=wv_rows[:].rearrange("p t n -> p n t"))
+            nc.vector.tensor_tensor(out=lin[:], in0=w1_bf[:], in1=wk_bf[:], op=ALU.subtract)
+            nc.vector.tensor_scalar(
+                out=quad[:], in0=wk_bf[:], scalar1=2.0, scalar2=None, op0=ALU.mult
+            )
+            nc.vector.tensor_copy(out=w0_f32[:], in_=w0_bf[:])
+            quantise((wv_codes, wv_scales), wv_grouped[:].rearrange("p n t -> p (n t)"))
+            nc.vector.tensor_scalar(
+                out=w0_ident[:], in0=ident[:], scalar1=w0_f32[:, 0:1], scalar2=None, op0=ALU.mult
+            )
 
-        def turn(bank, words, row_tile, first_word):
+        def turn(words, row_tile, first_word):
+            bank = psum_turn.tile([P, 2, 2 * P], F32, name="bank")
             for u in range(2):
                 for i in range(2):
                     nc.tensor.transpose(
@@ -121,27 +121,36 @@ def tile_gfsa_pa_t_kernel(tc, x, att, Wv, bv, w0, w1, wK, out):
                         words[:, row_tile + i, first_word + u * P : first_word + (u + 1) * P],
                         ident[:],
                     )
+            return bank
 
-        def prepare(b, j, t):
-            a_rows, x_rows = rows[b]
-            side, g = j // 2, j % 2
-            cols = slice(side * HALF, (side + 1) * HALF)
-
-            at_words = t["at_grouped"][:].bitcast(F32)
-            for pair in range(2 * side, 2 * side + 2):
-                bank = psum_turn.tile([P, 2, 2 * P], F32, name="bank")
-                turn(bank, a_rows[:].bitcast(F32), 2 * pair, g * (HALF // 2))
-                nc.scalar.copy(
-                    out=at_words[:, g, pair * 2 * P : (pair + 1) * 2 * P, :],
-                    in_=bank[:].rearrange("p u n -> p n u"),
+        def turn_att(n, i):
+            b, side, g = n // 4, n // 2 % 2, n % 2
+            if i == 0:
+                at_grouped[n] = sbuf.tile(
+                    [P, HALF, PACK], BF16, align_bytes=64, name="at_grouped", bufs=8
                 )
+            bank = turn(a_rows[b][:].bitcast(F32), 4 * side + 2 * i, g * (HALF // 2))
+            nc.scalar.copy(
+                out=at_grouped[n][:].bitcast(F32)[:, i * 2 * P : (i + 1) * 2 * P, :],
+                in_=bank[:].rearrange("p u n -> p n u"),
+            )
 
-            a_grouped = per_unit.tile([P, HALF, PACK], BF16, align_bytes=64, name="a_grouped")
+        def turn_x(n):
+            b, j = n // 4, n % 4
+            bank = turn(x_rows[b][:].bitcast(F32), 2 * j, 0)
+            xt_grouped[n] = sbuf.tile([P, 2 * P, PACK], BF16, align_bytes=64, name="xt_grouped")
+            nc.scalar.copy(
+                out=xt_grouped[n][:].bitcast(F32), in_=bank[:].rearrange("p u n -> p n u")
+            )
+
+        def regroup(n):
+            b, side, g = n // 4, n // 2 % 2, n % 2
+            a_grouped[n] = sbuf.tile([P, HALF, PACK], BF16, align_bytes=64, name="a_grouped")
 
             def key_block(i):
                 c = 2 * side + i
-                grouped = a_grouped[:, i * 2 * P : (i + 1) * 2 * P, :]
-                lying = a_rows[:, PACK * g : PACK * (g + 1), c * 2 * P : (c + 1) * 2 * P]
+                grouped = a_grouped[n][:, i * 2 * P : (i + 1) * 2 * P, :]
+                lying = a_rows[b][:, PACK * g : PACK * (g + 1), c * 2 * P : (c + 1) * 2 * P]
                 return (
                     grouped.rearrange("p (e q) t -> p e q t", e=2),
                     lying.rearrange("p t (q e) -> p e q t", e=2),
@@ -152,117 +161,146 @@ def tile_gfsa_pa_t_kernel(tc, x, att, Wv, bv, w0, w1, wK, out):
             grouped, lying = key_block(1)
             nc.scalar.copy(out=grouped, in_=lying)
 
-            bank = psum_turn.tile([P, 2, 2 * P], F32, name="bank")
-            turn(bank, x_rows[:].bitcast(F32), 2 * j, 0)
-            xt_grouped = per_unit.tile([P, 2 * P, PACK], BF16, align_bytes=64, name="xt_grouped")
-            nc.scalar.copy(out=xt_grouped[:].bitcast(F32), in_=bank[:].rearrange("p u n -> p n u"))
+        def quantise_at(n):
+            at_q[n] = operand("at", HALF, 8)
+            quantise(at_q[n], at_grouped[n][:].rearrange("p n t -> p (n t)"))
 
-            quantise(
-                t["at"][0][:, g, cols],
-                t["at"][1][:, g, cols],
-                t["at_grouped"][:, g, cols, :].rearrange("p n t -> p (n t)"),
-            )
-            quantise(
-                t["a"][0][:, g, cols],
-                t["a"][1][:, g, cols],
-                a_grouped[:].rearrange("p m t -> p (m t)"),
-            )
-            tokens = slice(j * 2 * P, (j + 1) * 2 * P)
-            quantise(
-                t["x"][0][:, tokens],
-                t["x"][1][:, tokens],
-                xt_grouped[:].rearrange("p n t -> p (n t)"),
-            )
+        def quantise_a(n):
+            a_q[n] = operand("a", HALF, 8)
+            quantise(a_q[n], a_grouped[n][:].rearrange("p m t -> p (m t)"))
 
-            if j % 2 == 1:
-                pas = j // 2
-                v_bank = psum_small.tile([P, PACK, DH], F32, name="small_bank")
-                for k in range(PACK):
-                    tile_cols = slice((PACK * pas + k) * P, (PACK * pas + k + 1) * P)
-                    mx(
-                        v_bank[:, k, :],
-                        (t["x"][0][:, tile_cols], t["x"][1][:, tile_cols]),
-                        (wv_codes[:], wv_scales[:]),
-                        True,
-                        True,
-                    )
-                v_grouped = per_unit.tile([P, DH, PACK], BF16, align_bytes=64, name="v_grouped")
-                nc.vector.tensor_tensor(
-                    out=v_grouped[:],
-                    in0=v_bank[:].rearrange("p t d -> p d t"),
-                    in1=bias[:].unsqueeze(2).to_broadcast([P, DH, PACK]),
-                    op=ALU.add,
-                )
-                quantise(
-                    t["v"][0][:, pas, :],
-                    t["v"][1][:, pas, :],
-                    v_grouped[:].rearrange("p d t -> p (d t)"),
-                )
+        def quantise_x(n):
+            x_q[n] = operand("x", 2 * P, 5)
+            quantise(x_q[n], xt_grouped[n][:].rearrange("p n t -> p (n t)"))
 
-        def finish(b, i, t):
-            side, pas = i // 2, i % 2
-            cols = slice(side * HALF, (side + 1) * HALF)
-
-            scaled = per_unit.tile([P, PACK, HALF], F32, name="scaled")
+        def values(n):
+            v_banks[n] = psum_small.tile([P, PACK, DH], F32, name="small_bank")
             for k in range(PACK):
-                key_cols = slice((PACK * pas + k) * P, (PACK * pas + k + 1) * P)
-                acc = psum_att2.tile([P, HALF], F32, name="acc")
-                for g in range(2):
-                    mx(
-                        acc[:],
-                        (t["a"][0][:, g, key_cols], t["a"][1][:, g, key_cols]),
-                        (t["at"][0][:, g, cols], t["at"][1][:, g, cols]),
-                        g == 0,
-                        g == 1,
-                    )
-                nc.scalar.activation(out=scaled[:, k, :], in_=acc[:], func=ACT.Copy, scale=quad[:, 0:1])
-                if side == pas:
-                    block = scaled[:, k, k * P : (k + 1) * P]
+                mx(
+                    v_banks[n][:, k, :],
+                    columns_of(x_q[n - 1 + k // 2], k % 2 * P, P),
+                    (wv_codes[:], wv_scales[:]),
+                    True,
+                    True,
+                )
+            v_grouped[n] = sbuf.tile([P, DH, PACK], BF16, align_bytes=64, name="v_grouped")
+            nc.vector.tensor_tensor(
+                out=v_grouped[n][:],
+                in0=v_banks[n][:].rearrange("p t d -> p d t"),
+                in1=bias[:].unsqueeze(2).to_broadcast([P, DH, PACK]),
+                op=ALU.add,
+            )
+
+        def quantise_v(n):
+            v_q[n] = operand("v", DH, 6)
+            quantise(v_q[n], v_grouped[n][:].rearrange("p d t -> p (d t)"))
+
+        def att2(n, k):
+            b, side, g = n // 4, n // 2 % 2, n % 2
+            if k == 0:
+                scaled[n] = sbuf.tile([P, PACK, HALF], F32, name="scaled")
+            acc = psum_att2.tile([P, HALF], F32, name="acc")
+            for c in range(2):
+                mx(
+                    acc[:],
+                    columns_of(a_q[4 * b + 2 * g + c], k * P, P),
+                    columns_of(at_q[4 * b + 2 * side + c], 0, HALF),
+                    c == 0,
+                    c == 1,
+                )
+            nc.scalar.activation(
+                out=scaled[n][:, k, :], in_=acc[:], func=ACT.Copy, scale=quad[:, 0:1]
+            )
+
+        def add_diagonal(n):
+            side, g = n // 2 % 2, n % 2
+            if side == g:
+                for k in range(PACK):
+                    block = scaled[n][:, k, k * P : (k + 1) * P]
                     nc.vector.tensor_tensor(out=block, in0=block, in1=w0_ident[:], op=ALU.add)
 
-            gf_grouped = per_unit.tile([P, HALF, PACK], BF16, align_bytes=64, name="gf_grouped")
+        def combine(n):
+            gf_grouped[n] = sbuf.tile([P, HALF, PACK], BF16, align_bytes=64, name="gf_grouped")
             nc.vector.scalar_tensor_tensor(
-                out=gf_grouped[:],
-                in0=t["at_grouped"][:, pas, cols, :],
+                out=gf_grouped[n][:],
+                in0=at_grouped[n][:],
                 scalar=lin[:, 0:1],
-                in1=scaled[:].rearrange("p t n -> p n t"),
+                in1=scaled[n][:].rearrange("p t n -> p n t"),
                 op0=ALU.mult,
                 op1=ALU.add,
             )
-            quantise(
-                t["gf"][0][:, pas, cols],
-                t["gf"][1][:, pas, cols],
-                gf_grouped[:].rearrange("p n t -> p (n t)"),
+
+        def quantise_gf(n):
+            gf_q[n] = operand("gf", HALF, 6)
+            quantise(gf_q[n], gf_grouped[n][:].rearrange("p n t -> p (n t)"))
+
+        def output(n):
+            b, side = n // 4, n // 2 % 2
+            o_bank = psum_small.tile([P, PACK, DH], F32, name="small_bank")
+            for k in range(PACK):
+                for g in range(2):
+                    mx(
+                        o_bank[:, k, :],
+                        columns_of(gf_q[n - 1 + g], k * P, P),
+                        columns_of(v_q[4 * b + 2 * g + 1], 0, DH),
+                        g == 0,
+                        g == 1,
+                    )
+            o_rows = sbuf.tile([P, PACK, DH], F32, name="o_rows")
+            nc.scalar.copy(out=o_rows[:], in_=o_bank[:])
+            nc.sync.dma_start(
+                out=out[b, side * HALF : (side + 1) * HALF, :].rearrange(
+                    "(u p e) d -> p u e d", p=P, e=2
+                ),
+                in_=o_rows[:].rearrange("p (u e) d -> p u e d", e=2),
             )
 
-            if pas == 1:
-                o_bank = psum_small.tile([P, PACK, DH], F32, name="small_bank")
-                for k in range(PACK):
-                    query_cols = slice((PACK * side + k) * P, (PACK * side + k + 1) * P)
-                    for g in range(2):
-                        mx(
-                            o_bank[:, k, :],
-                            (t["gf"][0][:, g, query_cols], t["gf"][1][:, g, query_cols]),
-                            (t["v"][0][:, g, :], t["v"][1][:, g, :]),
-                            g == 0,
-                            g == 1,
-                        )
-                o_rows = per_unit.tile([P, PACK, DH], F32, name="o_rows")
-                nc.scalar.copy(out=o_rows[:], in_=o_bank[:])
-                nc.sync.dma_start(
-                    out=out[b, cols, :].rearrange("(u p e) d -> p u e d", p=P, e=2),
-                    in_=o_rows[:].rearrange("p (u e) d -> p u e d", e=2),
-                )
+        def unit(step, lag):
+            return step - lag if 0 <= step - lag < UNITS else None
 
-        tiles = {}
-        for step in range(B * UNITS + LAG):
-            if step < B * UNITS:
-                b, j = divmod(step, UNITS)
-                if j == 0:
-                    tiles[b] = batch_tiles()
-                    if b + 1 < B:
-                        rows[b + 1] = load_batch(b + 1)
-                prepare(b, j, tiles[b])
-            if step >= LAG:
-                b, i = divmod(step - LAG, UNITS)
-                finish(b, i, tiles[b])
+        def second_unit(step, lag):
+            n = unit(step, lag)
+            return n if n is not None and n % 2 == 1 else None
+
+        for step in range(UNITS + OUT_LAG):
+            turned = unit(step, 0)
+            quantised = unit(step, QUANTISE_LAG)
+            valued = second_unit(step, VALUES_LAG)
+            squared = unit(step, ATT2_LAG)
+            combined = unit(step, COMBINE_LAG)
+            finished = second_unit(step, OUT_LAG)
+
+            if turned is not None and turned % 4 == 0 and turned // 4 + 1 < B:
+                load_batch(turned // 4 + 1)
+            if step == QUANTISE_LAG:
+                prepare_constants()
+            if combined is not None:
+                add_diagonal(combined)
+            if squared is not None:
+                att2(squared, 0)
+                att2(squared, 1)
+            if turned is not None:
+                turn_att(turned, 0)
+                turn_att(turned, 1)
+            if quantised is not None:
+                quantise_at(quantised)
+            if combined is not None:
+                combine(combined)
+            if quantised is not None:
+                quantise_a(quantised)
+            if combined is not None:
+                quantise_gf(combined)
+            if squared is not None:
+                att2(squared, 2)
+                att2(squared, 3)
+            if turned is not None:
+                turn_x(turned)
+                regroup(turned)
+            if valued is not None:
+                values(valued)
+            if quantised is not None:
+                quantise_x(quantised)
+            if valued is not None:
+                quantise_v(valued)
+            if finished is not None:
+                output(finished)

@@ -96,6 +96,7 @@ def tile_gfsa_pa_t_kernel(tc, x, att, Wv, bv, w0, w1, wK, out):
         quad = const.tile([P, 1], F32)
         w0_f32 = const.tile([P, 1], F32)
         w0_ident = const.tile([P, P], F32)
+        w0_masks = const.tile([P, PACK, P, PACK], BF16)
         wv_grouped = const.tile([P, DH, PACK], BF16, align_bytes=64)
         wv_codes = const.tile([P, DH], U32, align_bytes=64)
         wv_scales = const.tile([P, DH], U8, align_bytes=64)
@@ -108,9 +109,12 @@ def tile_gfsa_pa_t_kernel(tc, x, att, Wv, bv, w0, w1, wK, out):
             )
             nc.vector.tensor_copy(out=w0_f32[:], in_=w0_bf[:])
             quantise((wv_codes, wv_scales), wv_grouped[:].rearrange("p n t -> p (n t)"))
+            nc.vector.memset(w0_masks[:], 0.0)
             nc.vector.tensor_scalar(
                 out=w0_ident[:], in0=ident[:], scalar1=w0_f32[:, 0:1], scalar2=None, op0=ALU.mult
             )
+            for k in range(PACK):
+                nc.vector.tensor_copy(out=w0_masks[:, k, :, k], in_=w0_ident[:])
 
         def turn(words, row_tile, first_word):
             bank = psum_turn.tile([P, 2, 2 * P], F32, name="bank")
@@ -143,7 +147,7 @@ def tile_gfsa_pa_t_kernel(tc, x, att, Wv, bv, w0, w1, wK, out):
                 out=xt_grouped[n][:].bitcast(F32), in_=bank[:].rearrange("p u n -> p n u")
             )
 
-        def regroup(n):
+        def regroup(n, vector_helps):
             b, side, g = n // 4, n // 2 % 2, n % 2
             a_grouped[n] = sbuf.tile([P, HALF, PACK], BF16, align_bytes=64, name="a_grouped")
 
@@ -157,7 +161,10 @@ def tile_gfsa_pa_t_kernel(tc, x, att, Wv, bv, w0, w1, wK, out):
                 )
 
             grouped, lying = key_block(0)
-            nc.vector.tensor_copy(out=grouped, in_=lying)
+            if vector_helps:
+                nc.vector.tensor_copy(out=grouped, in_=lying)
+            else:
+                nc.scalar.copy(out=grouped, in_=lying)
             grouped, lying = key_block(1)
             nc.scalar.copy(out=grouped, in_=lying)
 
@@ -198,26 +205,34 @@ def tile_gfsa_pa_t_kernel(tc, x, att, Wv, bv, w0, w1, wK, out):
         def att2(n, k):
             b, side, g = n // 4, n // 2 % 2, n % 2
             if k == 0:
-                scaled[n] = sbuf.tile([P, PACK, HALF], F32, name="scaled")
-            acc = psum_att2.tile([P, HALF], F32, name="acc")
-            for c in range(2):
-                mx(
-                    acc[:],
-                    columns_of(a_q[4 * b + 2 * g + c], k * P, P),
-                    columns_of(at_q[4 * b + 2 * side + c], 0, HALF),
-                    c == 0,
-                    c == 1,
-                )
-            nc.scalar.activation(
-                out=scaled[n][:, k, :], in_=acc[:], func=ACT.Copy, scale=quad[:, 0:1]
-            )
-
-        def add_diagonal(n):
-            side, g = n // 2 % 2, n % 2
+                scaled[n] = sbuf.tile([P, HALF, PACK], F32, name="scaled")
+            acc = psum_att2.tile([P, PACK, P], F32, name="acc")
+            for t in range(PACK):
+                for c in range(2):
+                    mx(
+                        acc[:, t, :],
+                        columns_of(a_q[4 * b + 2 * g + c], t * P, P),
+                        columns_of(at_q[4 * b + 2 * side + c], k * P, P),
+                        c == 0,
+                        c == 1,
+                    )
+            words = scaled[n][:, k * P : (k + 1) * P, :]
             if side == g:
-                for k in range(PACK):
-                    block = scaled[n][:, k, k * P : (k + 1) * P]
-                    nc.vector.tensor_tensor(out=block, in0=block, in1=w0_ident[:], op=ALU.add)
+                nc.vector.scalar_tensor_tensor(
+                    out=words,
+                    in0=acc[:].rearrange("p t n -> p n t"),
+                    scalar=quad[:, 0:1],
+                    in1=w0_masks[:, k, :, :],
+                    op0=ALU.mult,
+                    op1=ALU.add,
+                )
+            else:
+                nc.scalar.activation(
+                    out=words,
+                    in_=acc[:].rearrange("p t n -> p n t"),
+                    func=ACT.Copy,
+                    scale=quad[:, 0:1],
+                )
 
         def combine(n):
             gf_grouped[n] = sbuf.tile([P, HALF, PACK], BF16, align_bytes=64, name="gf_grouped")
@@ -225,7 +240,7 @@ def tile_gfsa_pa_t_kernel(tc, x, att, Wv, bv, w0, w1, wK, out):
                 out=gf_grouped[n][:],
                 in0=at_grouped[n][:],
                 scalar=lin[:, 0:1],
-                in1=scaled[n][:].rearrange("p t n -> p n t"),
+                in1=scaled[n][:],
                 op0=ALU.mult,
                 op1=ALU.add,
             )
@@ -274,8 +289,6 @@ def tile_gfsa_pa_t_kernel(tc, x, att, Wv, bv, w0, w1, wK, out):
                 load_batch(turned // 4 + 1)
             if step == QUANTISE_LAG:
                 prepare_constants()
-            if combined is not None:
-                add_diagonal(combined)
             if squared is not None:
                 att2(squared, 0)
                 att2(squared, 1)
@@ -295,7 +308,7 @@ def tile_gfsa_pa_t_kernel(tc, x, att, Wv, bv, w0, w1, wK, out):
                 att2(squared, 3)
             if turned is not None:
                 turn_x(turned)
-                regroup(turned)
+                regroup(turned, squared is None)
             if valued is not None:
                 values(valued)
             if quantised is not None:

@@ -21,8 +21,9 @@ UNITS = 4 * B
 QUANTISE_LAG = 1
 VALUES_LAG = 2
 ATT2_LAG = 4
-COMBINE_LAG = 5
-OUT_LAG = 7
+LINEAR_LAG = 2
+GF_LAG = 5
+OUT_LAG = 6
 
 FLOPS = 2 * B * (N * D * DH + N * N * N + N * N * DH)
 
@@ -62,7 +63,7 @@ def tile_gfsa_pa_t_kernel(tc, x, att, Wv, bv, w0, w1, wK, out):
         a_rows, x_rows = {}, {}
         turn_banks, at_grouped, a_grouped, xt_grouped = {}, {}, {}, {}
         at_q, a_q, x_q, v_q, gf_q = {}, {}, {}, {}, {}
-        v_banks, v_grouped, scaled, gf_grouped = {}, {}, {}, {}
+        v_banks, v_grouped, linear, gf_grouped = {}, {}, {}, {}
 
         def load_batch(b):
             a_rows[b] = sbuf.tile([P, ROW_TILES, N], BF16, name="a_rows", bufs=2)
@@ -96,7 +97,6 @@ def tile_gfsa_pa_t_kernel(tc, x, att, Wv, bv, w0, w1, wK, out):
         quad = const.tile([P, 1], F32)
         w0_f32 = const.tile([P, 1], F32)
         w0_ident = const.tile([P, P], F32)
-        w0_masks = const.tile([P, PACK, P, PACK], BF16)
         wv_grouped = const.tile([P, DH, PACK], BF16, align_bytes=64)
         wv_codes = const.tile([P, DH], U32, align_bytes=64)
         wv_scales = const.tile([P, DH], U8, align_bytes=64)
@@ -109,12 +109,9 @@ def tile_gfsa_pa_t_kernel(tc, x, att, Wv, bv, w0, w1, wK, out):
             )
             nc.vector.tensor_copy(out=w0_f32[:], in_=w0_bf[:])
             quantise((wv_codes, wv_scales), wv_grouped[:].rearrange("p n t -> p (n t)"))
-            nc.vector.memset(w0_masks[:], 0.0)
             nc.vector.tensor_scalar(
                 out=w0_ident[:], in0=ident[:], scalar1=w0_f32[:, 0:1], scalar2=None, op0=ALU.mult
             )
-            for k in range(PACK):
-                nc.vector.tensor_copy(out=w0_masks[:, k, :, k], in_=w0_ident[:])
 
         def turn(words, row_tile, first_word):
             bank = psum_turn.tile([P, 2, 2 * P], F32, name="bank")
@@ -202,10 +199,41 @@ def tile_gfsa_pa_t_kernel(tc, x, att, Wv, bv, w0, w1, wK, out):
             v_q[n] = operand("v", DH, 6)
             quantise(v_q[n], v_grouped[n][:].rearrange("p d t -> p (d t)"))
 
+        def linear_part(n):
+            side, g = n // 2 % 2, n % 2
+            if side == g:
+                linear[n] = sbuf.tile([P, PACK, PACK, P], F32, name="linear_diagonal", bufs=2)
+                nc.scalar.activation(
+                    out=linear[n][:],
+                    in_=at_grouped[n][:].rearrange("p (k q) t -> p k t q", q=P),
+                    func=ACT.Copy,
+                    scale=lin[:, 0:1],
+                )
+                blocks = linear[n][:].rearrange("p k t q -> p (k t) q")[:, :: PACK + 1, :]
+                nc.gpsimd.tensor_tensor(
+                    out=blocks,
+                    in0=blocks,
+                    in1=w0_ident[:].unsqueeze(1).to_broadcast([P, PACK, P]),
+                    op=ALU.add,
+                )
+            else:
+                linear[n] = []
+                for k in range(PACK):
+                    part = sbuf.tile([P, P, PACK], F32, name="linear_part", bufs=8)
+                    nc.gpsimd.tensor_scalar(
+                        out=part[:],
+                        in0=at_grouped[n][:, k * P : (k + 1) * P, :],
+                        scalar1=lin[:, 0:1],
+                        scalar2=0.0,
+                        op0=ALU.mult,
+                        op1=ALU.add,
+                    )
+                    linear[n].append(part)
+
         def att2(n, k):
             b, side, g = n // 4, n // 2 % 2, n % 2
             if k == 0:
-                scaled[n] = sbuf.tile([P, HALF, PACK], F32, name="scaled")
+                gf_grouped[n] = sbuf.tile([P, HALF, PACK], BF16, align_bytes=64, name="gf_grouped")
             acc = psum_att2.tile([P, PACK, P], F32, name="acc")
             for t in range(PACK):
                 for c in range(2):
@@ -216,31 +244,15 @@ def tile_gfsa_pa_t_kernel(tc, x, att, Wv, bv, w0, w1, wK, out):
                         c == 0,
                         c == 1,
                     )
-            words = scaled[n][:, k * P : (k + 1) * P, :]
             if side == g:
-                nc.vector.scalar_tensor_tensor(
-                    out=words,
-                    in0=acc[:].rearrange("p t n -> p n t"),
-                    scalar=quad[:, 0:1],
-                    in1=w0_masks[:, k, :, :],
-                    op0=ALU.mult,
-                    op1=ALU.add,
-                )
+                part = linear[n][:, k, :, :].rearrange("p t q -> p q t")
             else:
-                nc.scalar.activation(
-                    out=words,
-                    in_=acc[:].rearrange("p t n -> p n t"),
-                    func=ACT.Copy,
-                    scale=quad[:, 0:1],
-                )
-
-        def combine(n):
-            gf_grouped[n] = sbuf.tile([P, HALF, PACK], BF16, align_bytes=64, name="gf_grouped")
+                part = linear[n][k][:]
             nc.vector.scalar_tensor_tensor(
-                out=gf_grouped[n][:],
-                in0=at_grouped[n][:],
-                scalar=lin[:, 0:1],
-                in1=scaled[n][:],
+                out=gf_grouped[n][:, k * P : (k + 1) * P, :],
+                in0=acc[:].rearrange("p t n -> p n t"),
+                scalar=quad[:, 0:1],
+                in1=part,
                 op0=ALU.mult,
                 op1=ALU.add,
             )
@@ -282,7 +294,8 @@ def tile_gfsa_pa_t_kernel(tc, x, att, Wv, bv, w0, w1, wK, out):
             quantised = unit(step, QUANTISE_LAG)
             valued = second_unit(step, VALUES_LAG)
             squared = unit(step, ATT2_LAG)
-            combined = unit(step, COMBINE_LAG)
+            linear_unit = unit(step, LINEAR_LAG)
+            completed = unit(step, GF_LAG)
             finished = second_unit(step, OUT_LAG)
 
             if turned is not None and turned % 4 == 0 and turned // 4 + 1 < B:
@@ -297,18 +310,18 @@ def tile_gfsa_pa_t_kernel(tc, x, att, Wv, bv, w0, w1, wK, out):
                 turn_att(turned, 1)
             if quantised is not None:
                 quantise_at(quantised)
-            if combined is not None:
-                combine(combined)
             if quantised is not None:
                 quantise_a(quantised)
-            if combined is not None:
-                quantise_gf(combined)
+            if completed is not None:
+                quantise_gf(completed)
             if squared is not None:
                 att2(squared, 2)
                 att2(squared, 3)
             if turned is not None:
                 turn_x(turned)
                 regroup(turned, squared is None)
+            if linear_unit is not None:
+                linear_part(linear_unit)
             if valued is not None:
                 values(valued)
             if quantised is not None:

@@ -16,15 +16,25 @@ P = 128
 PACK = 4
 HALF = 512
 ROW_TILES = N // P
-UNITS = 4 * B
+PARTS = 8
+TOTAL = PARTS * B
 
+X_LAG = 1
 QUANTISE_LAG = 1
-VALUES_LAG = 2
-ATT2_LAG = 4
-LINEAR_LAG = 2
-GF_LAG = 5
-OUT_LAG = 6
-
+ATT2_LAG = 6
+LINEAR_LEAD = 2
+GF_LAG = 7
+OUT_LAG = 8
+VALUES_LAG = 3
+FILL = 6
+LIN_ENG = "GG"
+DIAG_ENG = "S"
+ADD_ENG = "G"
+REG_V = "00000000"
+ROWBUFS = 3
+ACCB = 3
+TURNB = 3
+SMALLB = 2
 FLOPS = 2 * B * (N * D * DH + N * N * N + N * N * DH)
 
 
@@ -33,9 +43,9 @@ def tile_gfsa_pa_t_kernel(tc, x, att, Wv, bv, w0, w1, wK, out):
     with ExitStack() as ctx:
         const = ctx.enter_context(tc.tile_pool(name="const", bufs=1))
         sbuf = ctx.enter_context(tc.tile_pool(name="sbuf", bufs=3))
-        psum_turn = ctx.enter_context(tc.psum_pool(name="psum_turn", bufs=3))
-        psum_att2 = ctx.enter_context(tc.psum_pool(name="psum_att2", bufs=3))
-        psum_small = ctx.enter_context(tc.psum_pool(name="psum_small", bufs=2))
+        psum_turn = ctx.enter_context(tc.psum_pool(name="psum_turn", bufs=TURNB))
+        psum_att2 = ctx.enter_context(tc.psum_pool(name="psum_att2", bufs=ACCB))
+        psum_small = ctx.enter_context(tc.psum_pool(name="psum_small", bufs=SMALLB))
         ctx.enter_context(tc.manual_schedule())
 
         def operand(name, columns, bufs):
@@ -61,17 +71,19 @@ def tile_gfsa_pa_t_kernel(tc, x, att, Wv, bv, w0, w1, wK, out):
             )
 
         a_rows, x_rows = {}, {}
-        turn_banks, at_grouped, a_grouped, xt_grouped = {}, {}, {}, {}
+        at_grouped, a_grouped, xt_grouped = {}, {}, {}
         at_q, a_q, x_q, v_q, gf_q = {}, {}, {}, {}, {}
-        v_banks, v_grouped, linear, gf_grouped = {}, {}, {}, {}
+        v_grouped, linear, gf_grouped = {}, {}, {}
+        stores = []
 
         def load_batch(b):
-            a_rows[b] = sbuf.tile([P, ROW_TILES, N], BF16, name="a_rows", bufs=2)
-            x_rows[b] = sbuf.tile([P, ROW_TILES, D], BF16, name="x_rows", bufs=2)
+            a_rows[b] = sbuf.tile([P, ROW_TILES, N], BF16, name="a_rows", bufs=ROWBUFS)
+            x_rows[b] = sbuf.tile([P, ROW_TILES, D], BF16, name="x_rows", bufs=ROWBUFS)
             a_chunks = att[b, 0].rearrange("(c p e) m -> c p e m", p=P, e=2)
             x_chunks = x[b].rearrange("(c p e) d -> c p e d", p=P, e=2)
             for c in range(ROW_TILES // 2):
                 nc.sync.dma_start(out=a_rows[b][:, 2 * c : 2 * c + 2, :], in_=a_chunks[c])
+            for c in range(ROW_TILES // 2):
                 nc.sync.dma_start(out=x_rows[b][:, 2 * c : 2 * c + 2, :], in_=x_chunks[c])
 
         load_batch(0)
@@ -92,7 +104,6 @@ def tile_gfsa_pa_t_kernel(tc, x, att, Wv, bv, w0, w1, wK, out):
             out=wv_rows[:].rearrange("p (u e) n -> p u e n", e=2),
             in_=Wv.rearrange("(u p e) n -> p u e n", p=P, e=2),
         )
-
         lin = const.tile([P, 1], F32)
         quad = const.tile([P, 1], F32)
         w0_f32 = const.tile([P, 1], F32)
@@ -113,76 +124,64 @@ def tile_gfsa_pa_t_kernel(tc, x, att, Wv, bv, w0, w1, wK, out):
                 out=w0_ident[:], in0=ident[:], scalar1=w0_f32[:, 0:1], scalar2=None, op0=ALU.mult
             )
 
-        def turn(words, row_tile, first_word):
+        def transpose_words(bank_slice, words, row_tile, first_word):
+            nc.tensor.transpose(bank_slice, words[:, row_tile, first_word : first_word + P], ident[:])
+
+        def turn_att(n):
+            b, block, g = n // PARTS, n % PARTS // 2, n % 2
+            words = a_rows[b][:].bitcast(F32)
             bank = psum_turn.tile([P, 2, 2 * P], F32, name="bank")
             for u in range(2):
                 for i in range(2):
-                    nc.tensor.transpose(
-                        bank[:, u, i * P : (i + 1) * P],
-                        words[:, row_tile + i, first_word + u * P : first_word + (u + 1) * P],
-                        ident[:],
+                    transpose_words(
+                        bank[:, u, i * P : (i + 1) * P], words, 2 * block + i, (2 * g + u) * P
                     )
-            return bank
-
-        def turn_att(n, i):
-            b, side, g = n // 4, n // 2 % 2, n % 2
-            if i == 0:
-                at_grouped[n] = sbuf.tile(
-                    [P, HALF, PACK], BF16, align_bytes=64, name="at_grouped", bufs=8
-                )
-            bank = turn(a_rows[b][:].bitcast(F32), 4 * side + 2 * i, g * (HALF // 2))
+            at_grouped[n] = sbuf.tile([P, 2 * P, PACK], BF16, align_bytes=64, name="at_grouped", bufs=10)
             nc.scalar.copy(
-                out=at_grouped[n][:].bitcast(F32)[:, i * 2 * P : (i + 1) * 2 * P, :],
-                in_=bank[:].rearrange("p u n -> p n u"),
+                out=at_grouped[n][:].bitcast(F32), in_=bank[:].rearrange("p u n -> p n u")
             )
 
         def turn_x(n):
-            b, j = n // 4, n % 4
-            bank = turn(x_rows[b][:].bitcast(F32), 2 * j, 0)
-            xt_grouped[n] = sbuf.tile([P, 2 * P, PACK], BF16, align_bytes=64, name="xt_grouped")
+            b, r = n // PARTS, n % PARTS
+            words = x_rows[b][:].bitcast(F32)
+            bank = psum_turn.tile([P, 2, P], F32, name="bank")
+            for u in range(2):
+                transpose_words(bank[:, u, :], words, r, u * P)
+            xt_grouped[n] = sbuf.tile([P, P, PACK], BF16, align_bytes=64, name="xt_grouped")
             nc.scalar.copy(
                 out=xt_grouped[n][:].bitcast(F32), in_=bank[:].rearrange("p u n -> p n u")
             )
 
-        def regroup(n, vector_helps):
-            b, side, g = n // 4, n // 2 % 2, n % 2
-            a_grouped[n] = sbuf.tile([P, HALF, PACK], BF16, align_bytes=64, name="a_grouped")
-
-            def key_block(i):
-                c = 2 * side + i
-                grouped = a_grouped[n][:, i * 2 * P : (i + 1) * 2 * P, :]
-                lying = a_rows[b][:, PACK * g : PACK * (g + 1), c * 2 * P : (c + 1) * 2 * P]
-                return (
-                    grouped.rearrange("p (e q) t -> p e q t", e=2),
-                    lying.rearrange("p t (q e) -> p e q t", e=2),
-                )
-
-            grouped, lying = key_block(0)
-            if vector_helps:
+        def regroup(n, on_vector):
+            b, half, g, i = n // PARTS, n % PARTS // 4, n // 2 % 2, n % 2
+            c = 2 * half + i
+            a_grouped[n] = sbuf.tile([P, 2 * P, PACK], BF16, align_bytes=64, name="a_grouped")
+            lying = a_rows[b][:, PACK * g : PACK * (g + 1), c * 2 * P : (c + 1) * 2 * P]
+            grouped = a_grouped[n][:].rearrange("p (e q) t -> p e q t", e=2)
+            lying = lying.rearrange("p t (q e) -> p e q t", e=2)
+            if on_vector:
                 nc.vector.tensor_copy(out=grouped, in_=lying)
             else:
                 nc.scalar.copy(out=grouped, in_=lying)
-            grouped, lying = key_block(1)
-            nc.scalar.copy(out=grouped, in_=lying)
 
         def quantise_at(n):
-            at_q[n] = operand("at", HALF, 8)
+            at_q[n] = operand("at", 2 * P, 16)
             quantise(at_q[n], at_grouped[n][:].rearrange("p n t -> p (n t)"))
 
         def quantise_a(n):
-            a_q[n] = operand("a", HALF, 8)
+            a_q[n] = operand("a", 2 * P, 16)
             quantise(a_q[n], a_grouped[n][:].rearrange("p m t -> p (m t)"))
 
         def quantise_x(n):
-            x_q[n] = operand("x", 2 * P, 5)
+            x_q[n] = operand("x", P, 8)
             quantise(x_q[n], xt_grouped[n][:].rearrange("p n t -> p (n t)"))
 
         def values(n):
-            v_banks[n] = psum_small.tile([P, PACK, DH], F32, name="small_bank")
+            bank = psum_small.tile([P, PACK, DH], F32, name="small_bank")
             for k in range(PACK):
                 mx(
-                    v_banks[n][:, k, :],
-                    columns_of(x_q[n - 1 + k // 2], k % 2 * P, P),
+                    bank[:, k, :],
+                    columns_of(x_q[n - 3 + k], 0, P),
                     (wv_codes[:], wv_scales[:]),
                     True,
                     True,
@@ -190,143 +189,148 @@ def tile_gfsa_pa_t_kernel(tc, x, att, Wv, bv, w0, w1, wK, out):
             v_grouped[n] = sbuf.tile([P, DH, PACK], BF16, align_bytes=64, name="v_grouped")
             nc.vector.tensor_tensor(
                 out=v_grouped[n][:],
-                in0=v_banks[n][:].rearrange("p t d -> p d t"),
+                in0=bank[:].rearrange("p t d -> p d t"),
                 in1=bias[:].unsqueeze(2).to_broadcast([P, DH, PACK]),
                 op=ALU.add,
             )
 
         def quantise_v(n):
-            v_q[n] = operand("v", DH, 6)
+            v_q[n] = operand("v", DH, 4)
             quantise(v_q[n], v_grouped[n][:].rearrange("p d t -> p (d t)"))
 
+        def place(n):
+            return n // PARTS, n % PARTS // 4, n % 4
+
         def linear_part(n):
-            side, g = n // 2 % 2, n % 2
-            if side == g:
-                linear[n] = sbuf.tile([P, PACK, PACK, P], F32, name="linear_diagonal", bufs=2)
-                nc.scalar.activation(
-                    out=linear[n][:],
-                    in_=at_grouped[n][:].rearrange("p (k q) t -> p k t q", q=P),
-                    func=ACT.Copy,
-                    scale=lin[:, 0:1],
-                )
-                blocks = linear[n][:].rearrange("p k t q -> p (k t) q")[:, :: PACK + 1, :]
-                nc.gpsimd.tensor_tensor(
-                    out=blocks,
-                    in0=blocks,
-                    in1=w0_ident[:].unsqueeze(1).to_broadcast([P, PACK, P]),
-                    op=ALU.add,
-                )
+            b, g, block = place(n)
+            source = at_grouped[b * PARTS + 2 * block + g]
+            if block // 2 == g:
+                linear[n] = sbuf.tile([P, 2, PACK, P], F32, name="linear_diagonal", bufs=3)
+                src = source[:].rearrange("p (k q) t -> p k t q", q=P)
+                if DIAG_ENG == "S":
+                    nc.scalar.activation(out=linear[n][:], in_=src, func=ACT.Copy, scale=lin[:, 0:1])
+                elif DIAG_ENG == "V":
+                    nc.vector.tensor_scalar(out=linear[n][:], in0=src, scalar1=lin[:, 0:1], scalar2=None, op0=ALU.mult)
+                else:
+                    nc.gpsimd.tensor_scalar(out=linear[n][:], in0=src, scalar1=lin[:, 0:1], scalar2=0.0, op0=ALU.mult, op1=ALU.add)
+                first = 2 * (block % 2)
+                blocks = linear[n][:].rearrange("p k t q -> p (k t) q")[:, first : first + PACK + 2 : PACK + 1, :]
+                (nc.gpsimd if ADD_ENG == "G" else nc.vector).tensor_tensor(
+                    out=blocks, in0=blocks, in1=w0_ident[:].unsqueeze(1).to_broadcast([P, 2, P]), op=ALU.add)
             else:
                 linear[n] = []
-                for k in range(PACK):
-                    part = sbuf.tile([P, P, PACK], F32, name="linear_part", bufs=8)
-                    nc.gpsimd.tensor_scalar(
-                        out=part[:],
-                        in0=at_grouped[n][:, k * P : (k + 1) * P, :],
-                        scalar1=lin[:, 0:1],
-                        scalar2=0.0,
-                        op0=ALU.mult,
-                        op1=ALU.add,
-                    )
+                for k in range(2):
+                    part = sbuf.tile([P, P, PACK], F32, name="linear_part", bufs=6)
+                    src = source[:, k * P : (k + 1) * P, :]
+                    e = LIN_ENG[k]
+                    if e == "G":
+                        nc.gpsimd.tensor_scalar(out=part[:], in0=src, scalar1=lin[:, 0:1], scalar2=0.0, op0=ALU.mult, op1=ALU.add)
+                    elif e == "V":
+                        nc.vector.tensor_scalar(out=part[:], in0=src, scalar1=lin[:, 0:1], scalar2=None, op0=ALU.mult)
+                    else:
+                        nc.scalar.activation(out=part[:], in_=src, func=ACT.Copy, scale=lin[:, 0:1])
                     linear[n].append(part)
 
-        def att2(n, k):
-            b, side, g = n // 4, n // 2 % 2, n % 2
-            if k == 0:
-                gf_grouped[n] = sbuf.tile([P, HALF, PACK], BF16, align_bytes=64, name="gf_grouped")
-            acc = psum_att2.tile([P, PACK, P], F32, name="acc")
-            for t in range(PACK):
-                for c in range(2):
-                    mx(
-                        acc[:, t, :],
-                        columns_of(a_q[4 * b + 2 * g + c], t * P, P),
-                        columns_of(at_q[4 * b + 2 * side + c], k * P, P),
-                        c == 0,
-                        c == 1,
-                    )
-            if side == g:
-                part = linear[n][:, k, :, :].rearrange("p t q -> p q t")
-            else:
-                part = linear[n][k][:]
-            nc.vector.scalar_tensor_tensor(
-                out=gf_grouped[n][:, k * P : (k + 1) * P, :],
-                in0=acc[:].rearrange("p t n -> p n t"),
-                scalar=quad[:, 0:1],
-                in1=part,
-                op0=ALU.mult,
-                op1=ALU.add,
-            )
+        def att2(n):
+            b, g, block = place(n)
+            gf_grouped[n] = sbuf.tile([P, 2 * P, PACK], BF16, align_bytes=64, name="gf_grouped")
+            for k in range(2):
+                acc = psum_att2.tile([P, PACK, P], F32, name="acc")
+                for t in range(PACK):
+                    for c in range(2):
+                        mx(
+                            acc[:, t, :],
+                            columns_of(a_q[b * PARTS + 4 * g + 2 * c + t // 2], t % 2 * P, P),
+                            columns_of(at_q[b * PARTS + 2 * block + c], k * P, P),
+                            c == 0,
+                            c == 1,
+                        )
+                if block // 2 == g:
+                    part = linear[n][:, k, :, :].rearrange("p t q -> p q t")
+                else:
+                    part = linear[n][k][:]
+                nc.vector.scalar_tensor_tensor(
+                    out=gf_grouped[n][:, k * P : (k + 1) * P, :],
+                    in0=acc[:].rearrange("p t n -> p n t"),
+                    scalar=quad[:, 0:1],
+                    in1=part,
+                    op0=ALU.mult,
+                    op1=ALU.add,
+                )
 
         def quantise_gf(n):
-            gf_q[n] = operand("gf", HALF, 6)
+            gf_q[n] = operand("gf", 2 * P, 10)
             quantise(gf_q[n], gf_grouped[n][:].rearrange("p n t -> p (n t)"))
 
         def output(n):
-            b, side = n // 4, n // 2 % 2
-            o_bank = psum_small.tile([P, PACK, DH], F32, name="small_bank")
-            for k in range(PACK):
-                for g in range(2):
+            b, g, block = place(n)
+            bank = psum_small.tile([P, 2, DH], F32, name="small_bank")
+            for k in range(2):
+                for c in range(2):
                     mx(
-                        o_bank[:, k, :],
-                        columns_of(gf_q[n - 1 + g], k * P, P),
-                        columns_of(v_q[4 * b + 2 * g + 1], 0, DH),
-                        g == 0,
-                        g == 1,
+                        bank[:, k, :],
+                        columns_of(gf_q[n - 4 + 4 * c], k * P, P),
+                        columns_of(v_q[b * PARTS + 4 * c + 3], 0, DH),
+                        c == 0,
+                        c == 1,
                     )
-            o_rows = sbuf.tile([P, PACK, DH], F32, name="o_rows")
-            nc.scalar.copy(out=o_rows[:], in_=o_bank[:])
-            nc.sync.dma_start(
-                out=out[b, side * HALF : (side + 1) * HALF, :].rearrange(
-                    "(u p e) d -> p u e d", p=P, e=2
-                ),
-                in_=o_rows[:].rearrange("p (u e) d -> p u e d", e=2),
+            o_rows = sbuf.tile([P, 2, DH], F32, name="o_rows")
+            nc.scalar.copy(out=o_rows[:], in_=bank[:])
+            stores.append((b, block, o_rows))
+
+        def store():
+            b, block, o_rows = stores.pop()
+            nc.scalar.dma_start(
+                out=out[b, block * 2 * P : (block + 1) * 2 * P, :].rearrange("(p e) d -> p e d", e=2),
+                in_=o_rows[:],
             )
 
-        def unit(step, lag):
-            return step - lag if 0 <= step - lag < UNITS else None
+        def part(step, lag):
+            return step - lag if 0 <= step - lag < TOTAL else None
 
-        def second_unit(step, lag):
-            n = unit(step, lag)
-            return n if n is not None and n % 2 == 1 else None
-
-        for step in range(UNITS + OUT_LAG):
-            turned = unit(step, 0)
-            quantised = unit(step, QUANTISE_LAG)
-            valued = second_unit(step, VALUES_LAG)
-            squared = unit(step, ATT2_LAG)
-            linear_unit = unit(step, LINEAR_LAG)
-            completed = unit(step, GF_LAG)
-            finished = second_unit(step, OUT_LAG)
-
-            if turned is not None and turned % 4 == 0 and turned // 4 + 1 < B:
-                load_batch(turned // 4 + 1)
-            if step == QUANTISE_LAG:
+        for step in range(TOTAL + OUT_LAG + 1):
+            turned = part(step, 0)
+            quantised = part(step, QUANTISE_LAG)
+            x_turned = part(step, X_LAG)
+            x_quantised = part(step, X_LAG + 1)
+            valued = part(step, X_LAG + 2)
+            squared = part(step, ATT2_LAG)
+            lined = part(step, ATT2_LAG - LINEAR_LEAD)
+            completed = part(step, GF_LAG)
+            finished = part(step, OUT_LAG)
+            if turned is not None and turned % PARTS == 0 and turned // PARTS + 1 < B:
+                load_batch(turned // PARTS + 1)
+            if step == 1:
                 prepare_constants()
-            if squared is not None:
-                att2(squared, 0)
-                att2(squared, 1)
+            if stores:
+                store()
             if turned is not None:
-                turn_att(turned, 0)
-                turn_att(turned, 1)
+                regroup(turned, step < FILL or REG_V[turned % PARTS] == "1")
             if quantised is not None:
                 quantise_at(quantised)
-            if quantised is not None:
                 quantise_a(quantised)
-            if completed is not None:
-                quantise_gf(completed)
-            if squared is not None:
-                att2(squared, 2)
-                att2(squared, 3)
-            if turned is not None:
-                turn_x(turned)
-                regroup(turned, squared is None)
-            if linear_unit is not None:
-                linear_part(linear_unit)
-            if valued is not None:
-                values(valued)
-            if quantised is not None:
-                quantise_x(quantised)
-            if valued is not None:
-                quantise_v(valued)
-            if finished is not None:
-                output(finished)
+            if x_quantised is not None:
+                quantise_x(x_quantised)
+            vq = part(step, X_LAG + 3)
+            if vq is not None and vq % 4 == 3:
+                quantise_v(vq)
+            def do_att2():
+                if squared is not None:
+                    att2(squared)
+                if completed is not None:
+                    quantise_gf(completed)
+            def do_turn():
+                if turned is not None:
+                    turn_att(turned)
+                if x_turned is not None:
+                    turn_x(x_turned)
+            def do_v():
+                if valued is not None and valued % 4 == 3:
+                    values(valued)
+                if finished is not None and finished % PARTS >= 4:
+                    output(finished)
+            do_turn()
+            do_att2()
+            do_v()
+            if lined is not None:
+                linear_part(lined)

@@ -16,25 +16,24 @@ P = 128
 PACK = 4
 HALF = 512
 ROW_TILES = N // P
-PARTS = 8
-TOTAL = PARTS * B
+UNITS = 4 * B
 
-X_LAG = 1
-QUANTISE_LAG = 1
-ATT2_LAG = 6
-LINEAR_LEAD = 2
-GF_LAG = 7
-OUT_LAG = 8
-VALUES_LAG = 3
-FILL = 6
-LIN_ENG = "GG"
-DIAG_ENG = "S"
+X_LAG = 0
+ATT2_LAG = 3
+LIN_LEAD = 1
+FILL = 3
+FILL_V = 2
+LIN_ENG = "GGGG"
+DIAG_ENG = "GGGG"
 ADD_ENG = "G"
-REG_V = "00000000"
-ROWBUFS = 3
+REG = ["SS", "SS", "SS", "SS"]
+ROWBUFS = 2
 ACCB = 3
 TURNB = 3
 SMALLB = 2
+MERGE = 1
+V_ORDER = "qgx"
+PE_ORDER = "tavo"
 FLOPS = 2 * B * (N * D * DH + N * N * N + N * N * DH)
 
 
@@ -71,9 +70,8 @@ def tile_gfsa_pa_t_kernel(tc, x, att, Wv, bv, w0, w1, wK, out):
             )
 
         a_rows, x_rows = {}, {}
-        at_grouped, a_grouped, xt_grouped = {}, {}, {}
-        at_q, a_q, x_q, v_q, gf_q = {}, {}, {}, {}, {}
-        v_grouped, linear, gf_grouped = {}, {}, {}
+        grouped, codes, xt_grouped, x_q, v_grouped, v_q = {}, {}, {}, {}, {}, {}
+        linear, gf_grouped, gf_q = {}, {}, {}
         stores = []
 
         def load_batch(b):
@@ -90,6 +88,9 @@ def tile_gfsa_pa_t_kernel(tc, x, att, Wv, bv, w0, w1, wK, out):
 
         ident = const.tile([P, P], F32)
         make_identity(nc, ident[:])
+
+        ident_bf = const.tile([P, P], BF16)
+        make_identity(nc, ident_bf[:])
 
         w0_bf = const.tile([P, 1], BF16)
         w1_bf = const.tile([P, 1], BF16)
@@ -124,69 +125,82 @@ def tile_gfsa_pa_t_kernel(tc, x, att, Wv, bv, w0, w1, wK, out):
                 out=w0_ident[:], in0=ident[:], scalar1=w0_f32[:, 0:1], scalar2=None, op0=ALU.mult
             )
 
-        def transpose_words(bank_slice, words, row_tile, first_word):
-            nc.tensor.transpose(bank_slice, words[:, row_tile, first_word : first_word + P], ident[:])
+        def flat(ap):
+            return ap.rearrange("p n t -> p (n t)")
 
-        def turn_att(n):
-            b, block, g = n // PARTS, n % PARTS // 2, n % 2
-            words = a_rows[b][:].bitcast(F32)
+        def turn(words, row_tile, first_word):
             bank = psum_turn.tile([P, 2, 2 * P], F32, name="bank")
             for u in range(2):
                 for i in range(2):
-                    transpose_words(
-                        bank[:, u, i * P : (i + 1) * P], words, 2 * block + i, (2 * g + u) * P
+                    nc.tensor.transpose(
+                        bank[:, u, i * P : (i + 1) * P],
+                        words[:, row_tile + i, first_word + u * P : first_word + (u + 1) * P],
+                        ident[:],
                     )
-            at_grouped[n] = sbuf.tile([P, 2 * P, PACK], BF16, align_bytes=64, name="at_grouped", bufs=10)
-            nc.scalar.copy(
-                out=at_grouped[n][:].bitcast(F32), in_=bank[:].rearrange("p u n -> p n u")
-            )
+            return bank
+
+        def new_grouped(n):
+            grouped[n] = sbuf.tile([P, 2 * HALF, PACK], BF16, align_bytes=64, name="grouped", bufs=6)
+
+        def turn_att(n, c):
+            b, block = n // 4, n % 4
+            bank = turn(a_rows[b][:].bitcast(F32), 2 * block, c * 2 * P)
+            out_words = grouped[n][:, c * 2 * P : (c + 1) * 2 * P, :].bitcast(F32)
+            nc.scalar.copy(out=out_words, in_=bank[:].rearrange("p u n -> p n u"))
 
         def turn_x(n):
-            b, r = n // PARTS, n % PARTS
-            words = x_rows[b][:].bitcast(F32)
-            bank = psum_turn.tile([P, 2, P], F32, name="bank")
-            for u in range(2):
-                transpose_words(bank[:, u, :], words, r, u * P)
-            xt_grouped[n] = sbuf.tile([P, P, PACK], BF16, align_bytes=64, name="xt_grouped")
+            b, j = n // 4, n % 4
+            bank = turn(x_rows[b][:].bitcast(F32), 2 * j, 0)
+            xt_grouped[n] = sbuf.tile([P, 2 * P, PACK], BF16, align_bytes=64, name="xt_grouped")
             nc.scalar.copy(
                 out=xt_grouped[n][:].bitcast(F32), in_=bank[:].rearrange("p u n -> p n u")
             )
 
-        def regroup(n, on_vector):
-            b, half, g, i = n // PARTS, n % PARTS // 4, n // 2 % 2, n % 2
+        def regroup(n, i, engine):
+            b, half, g = n // 4, n % 4 // 2, n % 2
             c = 2 * half + i
-            a_grouped[n] = sbuf.tile([P, 2 * P, PACK], BF16, align_bytes=64, name="a_grouped")
             lying = a_rows[b][:, PACK * g : PACK * (g + 1), c * 2 * P : (c + 1) * 2 * P]
-            grouped = a_grouped[n][:].rearrange("p (e q) t -> p e q t", e=2)
             lying = lying.rearrange("p t (q e) -> p e q t", e=2)
-            if on_vector:
-                nc.vector.tensor_copy(out=grouped, in_=lying)
+            dest = grouped[n][:, HALF + i * 2 * P : HALF + (i + 1) * 2 * P, :]
+            dest = dest.rearrange("p (e q) t -> p e q t", e=2)
+            if engine == "P":
+                bank = psum_turn.tile([P, 2, P, PACK], BF16, name="bank")
+                for e in range(2):
+                    nc.tensor.matmul(
+                        out=bank[:, e, :, :], lhsT=ident_bf[:], rhs=lying[:, e, :, :], start=True, stop=True
+                    )
+                nc.scalar.copy(out=dest, in_=bank[:])
+            elif engine == "V":
+                nc.vector.tensor_copy(out=dest, in_=lying)
             else:
-                nc.scalar.copy(out=grouped, in_=lying)
+                nc.scalar.copy(out=dest, in_=lying)
 
-        def quantise_at(n):
-            at_q[n] = operand("at", 2 * P, 16)
-            quantise(at_q[n], at_grouped[n][:].rearrange("p n t -> p (n t)"))
-
-        def quantise_a(n):
-            a_q[n] = operand("a", 2 * P, 16)
-            quantise(a_q[n], a_grouped[n][:].rearrange("p m t -> p (m t)"))
+        def quantise_att(n):
+            codes[n] = operand("att", 2 * HALF, 9)
+            if MERGE:
+                quantise(codes[n], flat(grouped[n][:]))
+            else:
+                for i in range(2):
+                    quantise(
+                        (codes[n][0][:, i * HALF : (i + 1) * HALF], codes[n][1][:, i * HALF : (i + 1) * HALF]),
+                        flat(grouped[n][:, i * HALF : (i + 1) * HALF, :]),
+                    )
 
         def quantise_x(n):
-            x_q[n] = operand("x", P, 8)
-            quantise(x_q[n], xt_grouped[n][:].rearrange("p n t -> p (n t)"))
+            x_q[n] = operand("x", 2 * P, 4)
+            quantise(x_q[n], flat(xt_grouped[n][:]))
 
         def values(n):
             bank = psum_small.tile([P, PACK, DH], F32, name="small_bank")
             for k in range(PACK):
                 mx(
                     bank[:, k, :],
-                    columns_of(x_q[n - 3 + k], 0, P),
+                    columns_of(x_q[n - 1 + k // 2], k % 2 * P, P),
                     (wv_codes[:], wv_scales[:]),
                     True,
                     True,
                 )
-            v_grouped[n] = sbuf.tile([P, DH, PACK], BF16, align_bytes=64, name="v_grouped")
+            v_grouped[n] = sbuf.tile([P, DH, PACK], BF16, align_bytes=64, name="v_grouped", bufs=2)
             nc.vector.tensor_tensor(
                 out=v_grouped[n][:],
                 in0=bank[:].rearrange("p t d -> p d t"),
@@ -196,141 +210,156 @@ def tile_gfsa_pa_t_kernel(tc, x, att, Wv, bv, w0, w1, wK, out):
 
         def quantise_v(n):
             v_q[n] = operand("v", DH, 4)
-            quantise(v_q[n], v_grouped[n][:].rearrange("p d t -> p (d t)"))
+            quantise(v_q[n], flat(v_grouped[n][:]))
 
-        def place(n):
-            return n // PARTS, n % PARTS // 4, n % 4
+        def att_words(n, k):
+            b, side = n // 4, n % 2
+            return 4 * b + 2 * side + k // 2, n % 4 // 2
 
         def linear_part(n):
-            b, g, block = place(n)
-            source = at_grouped[b * PARTS + 2 * block + g]
-            if block // 2 == g:
-                linear[n] = sbuf.tile([P, 2, PACK, P], F32, name="linear_diagonal", bufs=3)
-                src = source[:].rearrange("p (k q) t -> p k t q", q=P)
-                if DIAG_ENG == "S":
-                    nc.scalar.activation(out=linear[n][:], in_=src, func=ACT.Copy, scale=lin[:, 0:1])
-                elif DIAG_ENG == "V":
-                    nc.vector.tensor_scalar(out=linear[n][:], in0=src, scalar1=lin[:, 0:1], scalar2=None, op0=ALU.mult)
-                else:
-                    nc.gpsimd.tensor_scalar(out=linear[n][:], in0=src, scalar1=lin[:, 0:1], scalar2=0.0, op0=ALU.mult, op1=ALU.add)
-                first = 2 * (block % 2)
-                blocks = linear[n][:].rearrange("p k t q -> p (k t) q")[:, first : first + PACK + 2 : PACK + 1, :]
-                (nc.gpsimd if ADD_ENG == "G" else nc.vector).tensor_tensor(
-                    out=blocks, in0=blocks, in1=w0_ident[:].unsqueeze(1).to_broadcast([P, 2, P]), op=ALU.add)
+            b, g, side = n // 4, n % 4 // 2, n % 2
+            if side == g:
+                linear[n] = sbuf.tile([P, PACK, PACK, P], F32, name="linear_diagonal", bufs=2)
+                for k in range(PACK):
+                    u = 4 * b + 2 * side + k // 2
+                    first = g * 2 * P + k % 2 * P
+                    src = grouped[u][:, first : first + P, :].rearrange("p q t -> p t q")
+                    scale_by(DIAG_ENG[k], linear[n][:, k, :, :], src)
+                if ADD_ENG == "G":
+                    add_identity(n)
             else:
                 linear[n] = []
-                for k in range(2):
-                    part = sbuf.tile([P, P, PACK], F32, name="linear_part", bufs=6)
-                    src = source[:, k * P : (k + 1) * P, :]
-                    e = LIN_ENG[k]
-                    if e == "G":
-                        nc.gpsimd.tensor_scalar(out=part[:], in0=src, scalar1=lin[:, 0:1], scalar2=0.0, op0=ALU.mult, op1=ALU.add)
-                    elif e == "V":
-                        nc.vector.tensor_scalar(out=part[:], in0=src, scalar1=lin[:, 0:1], scalar2=None, op0=ALU.mult)
-                    else:
-                        nc.scalar.activation(out=part[:], in_=src, func=ACT.Copy, scale=lin[:, 0:1])
+                for k in range(PACK):
+                    u = 4 * b + 2 * side + k // 2
+                    first = g * 2 * P + k % 2 * P
+                    part = sbuf.tile([P, P, PACK], F32, name="linear_part", bufs=8)
+                    scale_by(LIN_ENG[k], part[:], grouped[u][:, first : first + P, :])
                     linear[n].append(part)
 
-        def att2(n):
-            b, g, block = place(n)
-            gf_grouped[n] = sbuf.tile([P, 2 * P, PACK], BF16, align_bytes=64, name="gf_grouped")
-            for k in range(2):
-                acc = psum_att2.tile([P, PACK, P], F32, name="acc")
-                for t in range(PACK):
-                    for c in range(2):
-                        mx(
-                            acc[:, t, :],
-                            columns_of(a_q[b * PARTS + 4 * g + 2 * c + t // 2], t % 2 * P, P),
-                            columns_of(at_q[b * PARTS + 2 * block + c], k * P, P),
-                            c == 0,
-                            c == 1,
-                        )
-                if block // 2 == g:
-                    part = linear[n][:, k, :, :].rearrange("p t q -> p q t")
-                else:
-                    part = linear[n][k][:]
-                nc.vector.scalar_tensor_tensor(
-                    out=gf_grouped[n][:, k * P : (k + 1) * P, :],
-                    in0=acc[:].rearrange("p t n -> p n t"),
-                    scalar=quad[:, 0:1],
-                    in1=part,
-                    op0=ALU.mult,
-                    op1=ALU.add,
-                )
+        def scale_by(engine, dest, src):
+            if engine == "G":
+                nc.gpsimd.tensor_scalar(out=dest, in0=src, scalar1=lin[:, 0:1], scalar2=0.0, op0=ALU.mult, op1=ALU.add)
+            elif engine == "V":
+                nc.vector.tensor_scalar(out=dest, in0=src, scalar1=lin[:, 0:1], scalar2=None, op0=ALU.mult)
+            else:
+                nc.scalar.activation(out=dest, in_=src, func=ACT.Copy, scale=lin[:, 0:1])
 
-        def quantise_gf(n):
-            gf_q[n] = operand("gf", 2 * P, 10)
-            quantise(gf_q[n], gf_grouped[n][:].rearrange("p n t -> p (n t)"))
+        def add_identity(n):
+            if n % 2 == n % 4 // 2:
+                blocks = linear[n][:].rearrange("p k t q -> p (k t) q")[:, :: PACK + 1, :]
+                (nc.gpsimd if ADD_ENG == "G" else nc.vector).tensor_tensor(
+                    out=blocks, in0=blocks, in1=w0_ident[:].unsqueeze(1).to_broadcast([P, PACK, P]), op=ALU.add)
 
-        def output(n):
-            b, g, block = place(n)
-            bank = psum_small.tile([P, 2, DH], F32, name="small_bank")
-            for k in range(2):
+        def att2(n, k):
+            b, g, side = n // 4, n % 4 // 2, n % 2
+            if k == 0:
+                gf_grouped[n] = sbuf.tile([P, HALF, PACK], BF16, align_bytes=64, name="gf_grouped", bufs=2)
+            acc = psum_att2.tile([P, PACK, P], F32, name="acc")
+            for t in range(PACK):
                 for c in range(2):
                     mx(
-                        bank[:, k, :],
-                        columns_of(gf_q[n - 4 + 4 * c], k * P, P),
-                        columns_of(v_q[b * PARTS + 4 * c + 3], 0, DH),
+                        acc[:, t, :],
+                        columns_of(codes[4 * b + 2 * g + c], HALF + t * P, P),
+                        columns_of(codes[4 * b + 2 * side + k // 2], c * 2 * P + k % 2 * P, P),
                         c == 0,
                         c == 1,
                     )
-            o_rows = sbuf.tile([P, 2, DH], F32, name="o_rows")
-            nc.scalar.copy(out=o_rows[:], in_=bank[:])
-            stores.append((b, block, o_rows))
-
-        def store():
-            b, block, o_rows = stores.pop()
-            nc.scalar.dma_start(
-                out=out[b, block * 2 * P : (block + 1) * 2 * P, :].rearrange("(p e) d -> p e d", e=2),
-                in_=o_rows[:],
+            if side == g:
+                part = linear[n][:, k, :, :].rearrange("p t q -> p q t")
+            else:
+                part = linear[n][k][:]
+            nc.vector.scalar_tensor_tensor(
+                out=gf_grouped[n][:, k * P : (k + 1) * P, :],
+                in0=acc[:].rearrange("p t n -> p n t"),
+                scalar=quad[:, 0:1],
+                in1=part,
+                op0=ALU.mult,
+                op1=ALU.add,
             )
 
-        def part(step, lag):
-            return step - lag if 0 <= step - lag < TOTAL else None
+        def quantise_gf(n):
+            gf_q[n] = operand("gf", HALF, 4)
+            quantise(gf_q[n], flat(gf_grouped[n][:]))
 
-        for step in range(TOTAL + OUT_LAG + 1):
-            turned = part(step, 0)
-            quantised = part(step, QUANTISE_LAG)
-            x_turned = part(step, X_LAG)
-            x_quantised = part(step, X_LAG + 1)
-            valued = part(step, X_LAG + 2)
-            squared = part(step, ATT2_LAG)
-            lined = part(step, ATT2_LAG - LINEAR_LEAD)
-            completed = part(step, GF_LAG)
-            finished = part(step, OUT_LAG)
-            if turned is not None and turned % PARTS == 0 and turned // PARTS + 1 < B:
-                load_batch(turned // PARTS + 1)
+        def output(n):
+            b, side = n // 4, n % 2
+            bank = psum_small.tile([P, PACK, DH], F32, name="small_bank")
+            for k in range(PACK):
+                for c in range(2):
+                    mx(
+                        bank[:, k, :],
+                        columns_of(gf_q[n - 2 + 2 * c], k * P, P),
+                        columns_of(v_q[4 * b + 2 * c + 1], 0, DH),
+                        c == 0,
+                        c == 1,
+                    )
+            o_rows = sbuf.tile([P, PACK, DH], F32, name="o_rows", bufs=2)
+            nc.scalar.copy(out=o_rows[:], in_=bank[:])
+            stores.append((b, side, o_rows))
+
+        def store():
+            b, side, o_rows = stores.pop()
+            nc.scalar.dma_start(
+                out=out[b, side * HALF : (side + 1) * HALF, :].rearrange("(u p e) d -> p u e d", p=P, e=2),
+                in_=o_rows[:].rearrange("p (u e) d -> p u e d", e=2),
+            )
+
+        def unit(step, lag):
+            return step - lag if 0 <= step - lag < UNITS else None
+
+        for step in range(UNITS + ATT2_LAG + 2):
+            turned = unit(step, 0)
+            quantised = unit(step, 1)
+            x_turned = unit(step, X_LAG)
+            x_quantised = unit(step, X_LAG + 1)
+            valued = unit(step, X_LAG + 2)
+            v_quantised = unit(step, X_LAG + 3)
+            lined = unit(step, ATT2_LAG - LIN_LEAD)
+            added = unit(step, ATT2_LAG)
+            squared = unit(step, ATT2_LAG)
+            completed = unit(step, ATT2_LAG + 1)
+            if turned is not None and turned % 4 == 0 and turned // 4 + 1 < B:
+                load_batch(turned // 4 + 1)
             if step == 1:
                 prepare_constants()
+            if turned is not None:
+                new_grouped(turned)
+                ways = REG[turned % 4]
+                if step < FILL:
+                    ways = ("V" * FILL_V + ways)[:2]
+                for i in range(2):
+                    if ways[i] != "P":
+                        regroup(turned, i, ways[i])
             if stores:
                 store()
-            if turned is not None:
-                regroup(turned, step < FILL or REG_V[turned % PARTS] == "1")
-            if quantised is not None:
-                quantise_at(quantised)
-                quantise_a(quantised)
-            if x_quantised is not None:
-                quantise_x(x_quantised)
-            vq = part(step, X_LAG + 3)
-            if vq is not None and vq % 4 == 3:
-                quantise_v(vq)
-            def do_att2():
-                if squared is not None:
-                    att2(squared)
-                if completed is not None:
+            for ch in V_ORDER:
+                if ch == "g" and completed is not None:
                     quantise_gf(completed)
-            def do_turn():
-                if turned is not None:
-                    turn_att(turned)
-                if x_turned is not None:
-                    turn_x(x_turned)
-            def do_v():
-                if valued is not None and valued % 4 == 3:
+                if ch == "q" and quantised is not None:
+                    quantise_att(quantised)
+                if ch == "x":
+                    if x_quantised is not None:
+                        quantise_x(x_quantised)
+                    if v_quantised is not None and v_quantised % 2 == 1:
+                        quantise_v(v_quantised)
+                    if ADD_ENG == "V" and added is not None:
+                        add_identity(added)
+            for ch in PE_ORDER:
+                if ch == "t":
+                    if turned is not None:
+                        turn_att(turned, 0)
+                        turn_att(turned, 1)
+                        for i in range(2):
+                            if ways[i] == "P":
+                                regroup(turned, i, "P")
+                    if x_turned is not None:
+                        turn_x(x_turned)
+                if ch == "a" and squared is not None:
+                    for k in range(PACK):
+                        att2(squared, k)
+                if ch == "v" and valued is not None and valued % 2 == 1:
                     values(valued)
-                if finished is not None and finished % PARTS >= 4:
-                    output(finished)
-            do_turn()
-            do_att2()
-            do_v()
+                if ch == "o" and completed is not None and completed % 4 >= 2:
+                    output(completed)
             if lined is not None:
                 linear_part(lined)

@@ -24,7 +24,7 @@ LIN_LEAD = 1
 FILL = 3
 FILL_V = 2
 LIN_ENG = "GGGG"
-DIAG_ENG = "GGGG"
+DIAG_ENG = "GGSS"
 ADD_ENG = "G"
 REG = ["SS", "SS", "SS", "SS"]
 ROWBUFS = 2
@@ -32,7 +32,9 @@ ACCB = 3
 TURNB = 3
 SMALLB = 2
 MERGE = 1
-V_ORDER = "qgx"
+EARLY = 1
+DRAIN = 1
+V_ORDER = "qxg"
 PE_ORDER = "tavo"
 FLOPS = 2 * B * (N * D * DH + N * N * N + N * N * DH)
 
@@ -72,7 +74,7 @@ def tile_gfsa_pa_t_kernel(tc, x, att, Wv, bv, w0, w1, wK, out):
         a_rows, x_rows = {}, {}
         grouped, codes, xt_grouped, x_q, v_grouped, v_q = {}, {}, {}, {}, {}, {}
         linear, gf_grouped, gf_q = {}, {}, {}
-        stores = []
+        stores, banks = [], []
 
         def load_batch(b):
             a_rows[b] = sbuf.tile([P, ROW_TILES, N], BF16, name="a_rows", bufs=ROWBUFS)
@@ -216,25 +218,26 @@ def tile_gfsa_pa_t_kernel(tc, x, att, Wv, bv, w0, w1, wK, out):
             b, side = n // 4, n % 2
             return 4 * b + 2 * side + k // 2, n % 4 // 2
 
-        def linear_part(n):
+        def linear_part(n, who):
             b, g, side = n // 4, n % 4 // 2, n % 2
             if side == g:
-                linear[n] = sbuf.tile([P, PACK, PACK, P], F32, name="linear_diagonal", bufs=2)
+                if "S" in who:
+                    linear[n] = sbuf.tile([P, PACK, PACK, P], F32, align_bytes=64, name="linear_or_gf", bufs=3)
                 for k in range(PACK):
                     u = 4 * b + 2 * side + k // 2
                     first = g * 2 * P + k % 2 * P
                     src = grouped[u][:, first : first + P, :].rearrange("p q t -> p t q")
+                    if DIAG_ENG[k] not in who:
+                        continue
                     scale_by(DIAG_ENG[k], linear[n][:, k, :, :], src)
-                if ADD_ENG == "G":
+                if ADD_ENG == "G" and "G" in who:
                     add_identity(n)
             else:
-                linear[n] = []
+                linear[n] = sbuf.tile([P, PACK, P, PACK], F32, align_bytes=64, name="linear_or_gf", bufs=3)
                 for k in range(PACK):
                     u = 4 * b + 2 * side + k // 2
                     first = g * 2 * P + k % 2 * P
-                    part = sbuf.tile([P, P, PACK], F32, name="linear_part", bufs=8)
-                    scale_by(LIN_ENG[k], part[:], grouped[u][:, first : first + P, :])
-                    linear[n].append(part)
+                    scale_by(LIN_ENG[k], linear[n][:, k, :, :], grouped[u][:, first : first + P, :])
 
         def scale_by(engine, dest, src):
             if engine == "G":
@@ -252,8 +255,6 @@ def tile_gfsa_pa_t_kernel(tc, x, att, Wv, bv, w0, w1, wK, out):
 
         def att2(n, k):
             b, g, side = n // 4, n % 4 // 2, n % 2
-            if k == 0:
-                gf_grouped[n] = sbuf.tile([P, HALF, PACK], BF16, align_bytes=64, name="gf_grouped", bufs=2)
             acc = psum_att2.tile([P, PACK, P], F32, name="acc")
             for t in range(PACK):
                 for c in range(2):
@@ -267,7 +268,7 @@ def tile_gfsa_pa_t_kernel(tc, x, att, Wv, bv, w0, w1, wK, out):
             if side == g:
                 part = linear[n][:, k, :, :].rearrange("p t q -> p q t")
             else:
-                part = linear[n][k][:]
+                part = linear[n][:, k, :, :]
             nc.vector.scalar_tensor_tensor(
                 out=gf_grouped[n][:, k * P : (k + 1) * P, :],
                 in0=acc[:].rearrange("p t n -> p n t"),
@@ -293,6 +294,10 @@ def tile_gfsa_pa_t_kernel(tc, x, att, Wv, bv, w0, w1, wK, out):
                         c == 0,
                         c == 1,
                     )
+            banks.append((b, side, bank))
+
+        def drain():
+            b, side, bank = banks.pop()
             o_rows = sbuf.tile([P, PACK, DH], F32, name="o_rows", bufs=2)
             nc.scalar.copy(out=o_rows[:], in_=bank[:])
             stores.append((b, side, o_rows))
@@ -322,6 +327,12 @@ def tile_gfsa_pa_t_kernel(tc, x, att, Wv, bv, w0, w1, wK, out):
                 load_batch(turned // 4 + 1)
             if step == 1:
                 prepare_constants()
+            if squared is not None:
+                gf_grouped[squared] = sbuf.tile([P, HALF, PACK], BF16, align_bytes=64, name="linear_or_gf", bufs=3)
+            if DRAIN == 0 and banks:
+                drain()
+            if EARLY and lined is not None and lined % 2 == lined % 4 // 2:
+                linear_part(lined, "S")
             if turned is not None:
                 new_grouped(turned)
                 ways = REG[turned % 4]
@@ -330,8 +341,8 @@ def tile_gfsa_pa_t_kernel(tc, x, att, Wv, bv, w0, w1, wK, out):
                 for i in range(2):
                     if ways[i] != "P":
                         regroup(turned, i, ways[i])
-            if stores:
-                store()
+            if DRAIN == 1 and banks:
+                drain()
             for ch in V_ORDER:
                 if ch == "g" and completed is not None:
                     quantise_gf(completed)
@@ -361,5 +372,7 @@ def tile_gfsa_pa_t_kernel(tc, x, att, Wv, bv, w0, w1, wK, out):
                     values(valued)
                 if ch == "o" and completed is not None and completed % 4 >= 2:
                     output(completed)
+            if stores:
+                store()
             if lined is not None:
-                linear_part(lined)
+                linear_part(lined, "G" if EARLY and lined % 2 == lined % 4 // 2 else "SG")

@@ -23,7 +23,7 @@ ATT2_LAG = 3
 LIN_LEAD = 1
 FILL = 3
 FILL_V = 2
-LIN_ENG = "GGGG"
+LIN_ENG = "GGGS"
 DIAG_ENG = "GGSS"
 ADD_ENG = "G"
 REG = ["SS", "SS", "SS", "SS"]
@@ -32,6 +32,10 @@ ACCB = 3
 TURNB = 3
 SMALLB = 2
 MERGE = 1
+REGROUP_LATE = 1
+X_FIRST = 1
+CONST_STEP = 1
+W_STEP = 2
 EARLY = 1
 DRAIN = 1
 V_ORDER = "qxg"
@@ -115,14 +119,16 @@ def tile_gfsa_pa_t_kernel(tc, x, att, Wv, bv, w0, w1, wK, out):
         wv_codes = const.tile([P, DH], U32, align_bytes=64)
         wv_scales = const.tile([P, DH], U8, align_bytes=64)
 
-        def prepare_constants():
+        def prepare_weights():
             nc.vector.tensor_copy(out=wv_grouped[:], in_=wv_rows[:].rearrange("p t n -> p n t"))
+            quantise((wv_codes, wv_scales), wv_grouped[:].rearrange("p n t -> p (n t)"))
+
+        def prepare_constants():
             nc.vector.tensor_tensor(out=lin[:], in0=w1_bf[:], in1=wk_bf[:], op=ALU.subtract)
             nc.vector.tensor_scalar(
                 out=quad[:], in0=wk_bf[:], scalar1=2.0, scalar2=None, op0=ALU.mult
             )
             nc.vector.tensor_copy(out=w0_f32[:], in_=w0_bf[:])
-            quantise((wv_codes, wv_scales), wv_grouped[:].rearrange("p n t -> p (n t)"))
             nc.vector.tensor_scalar(
                 out=w0_ident[:], in0=ident[:], scalar1=w0_f32[:, 0:1], scalar2=None, op0=ALU.mult
             )
@@ -325,14 +331,19 @@ def tile_gfsa_pa_t_kernel(tc, x, att, Wv, bv, w0, w1, wK, out):
             completed = unit(step, ATT2_LAG + 1)
             if turned is not None and turned % 4 == 0 and turned // 4 + 1 < B:
                 load_batch(turned // 4 + 1)
-            if step == 1:
+            if step == CONST_STEP:
                 prepare_constants()
+            if step == W_STEP:
+                prepare_weights()
             if squared is not None:
                 gf_grouped[squared] = sbuf.tile([P, HALF, PACK], BF16, align_bytes=64, name="linear_or_gf", bufs=3)
             if DRAIN == 0 and banks:
                 drain()
             if EARLY and lined is not None and lined % 2 == lined % 4 // 2:
                 linear_part(lined, "S")
+            if REGROUP_LATE and step < FILL and quantised is not None:
+                quantise_att(quantised)
+                quantised = None
             if turned is not None:
                 new_grouped(turned)
                 ways = REG[turned % 4]
@@ -349,7 +360,10 @@ def tile_gfsa_pa_t_kernel(tc, x, att, Wv, bv, w0, w1, wK, out):
                 if ch == "q" and quantised is not None:
                     quantise_att(quantised)
                 if ch == "x":
-                    if x_quantised is not None:
+                    if x_quantised is not None and step > X_FIRST:
+                        if step == X_FIRST + 1:
+                            for j in range(X_FIRST):
+                                quantise_x(j)
                         quantise_x(x_quantised)
                     if v_quantised is not None and v_quantised % 2 == 1:
                         quantise_v(v_quantised)
@@ -363,7 +377,10 @@ def tile_gfsa_pa_t_kernel(tc, x, att, Wv, bv, w0, w1, wK, out):
                         for i in range(2):
                             if ways[i] == "P":
                                 regroup(turned, i, "P")
-                    if x_turned is not None:
+                    if x_turned is not None and step >= X_FIRST:
+                        if step == X_FIRST:
+                            for j in range(X_FIRST):
+                                turn_x(j)
                         turn_x(x_turned)
                 if ch == "a" and squared is not None:
                     for k in range(PACK):

@@ -24,7 +24,7 @@ LIN_LEAD = 1
 FILL = 3
 FILL_V = 2
 LIN_ENG = "GGGS"
-DIAG_ENG = "GGSS"
+PAIR_ENG = "GS"
 ADD_ENG = "G"
 REG = ["SS", "SS", "SS", "SS"]
 ROWBUFS = 2
@@ -228,15 +228,13 @@ def tile_gfsa_pa_t_kernel(tc, x, att, Wv, bv, w0, w1, wK, out):
             b, g, side = n // 4, n % 4 // 2, n % 2
             if side == g:
                 if "S" in who:
-                    linear[n] = sbuf.tile([P, PACK, PACK, P], F32, align_bytes=64, name="linear_or_gf", bufs=3)
-                for k in range(PACK):
-                    u = 4 * b + 2 * side + k // 2
-                    first = g * 2 * P + k % 2 * P
-                    src = grouped[u][:, first : first + P, :].rearrange("p q t -> p t q")
-                    if DIAG_ENG[k] not in who:
+                    linear[n] = sbuf.tile([P, 2, P, PACK, 2], F32, align_bytes=64, name="linear_or_gf", bufs=3)
+                for u in range(2):
+                    if PAIR_ENG[u] not in who:
                         continue
-                    scale_by(DIAG_ENG[k], linear[n][:, k, :, :], src)
-                if ADD_ENG == "G" and "G" in who:
+                    source = grouped[4 * b + 2 * side + u][:, g * 2 * P : (g + 1) * 2 * P, :]
+                    scale_by(PAIR_ENG[u], linear[n][:, u], source.rearrange("p (h q) t -> p q t h", h=2))
+                if "G" in who:
                     add_identity(n)
             else:
                 linear[n] = sbuf.tile([P, PACK, P, PACK], F32, align_bytes=64, name="linear_or_gf", bufs=3)
@@ -254,10 +252,11 @@ def tile_gfsa_pa_t_kernel(tc, x, att, Wv, bv, w0, w1, wK, out):
                 nc.scalar.activation(out=dest, in_=src, func=ACT.Copy, scale=lin[:, 0:1])
 
         def add_identity(n):
-            if n % 2 == n % 4 // 2:
-                blocks = linear[n][:].rearrange("p k t q -> p (k t) q")[:, :: PACK + 1, :]
-                (nc.gpsimd if ADD_ENG == "G" else nc.vector).tensor_tensor(
-                    out=blocks, in0=blocks, in1=w0_ident[:].unsqueeze(1).to_broadcast([P, PACK, P]), op=ALU.add)
+            for u in range(2):
+                pair = linear[n][:, u].rearrange("p q t h -> p q (t h)")
+                blocks = pair[:, :, PACK * u : PACK * u + PACK : 3]
+                nc.gpsimd.tensor_tensor(
+                    out=blocks, in0=blocks, in1=w0_ident[:].unsqueeze(2).to_broadcast([P, P, 2]), op=ALU.add)
 
         def att2(n, k):
             b, g, side = n // 4, n % 4 // 2, n % 2
@@ -272,7 +271,7 @@ def tile_gfsa_pa_t_kernel(tc, x, att, Wv, bv, w0, w1, wK, out):
                         c == 1,
                     )
             if side == g:
-                part = linear[n][:, k, :, :].rearrange("p t q -> p q t")
+                part = linear[n][:, k // 2, :, :, k % 2]
             else:
                 part = linear[n][:, k, :, :]
             nc.vector.scalar_tensor_tensor(
@@ -367,8 +366,6 @@ def tile_gfsa_pa_t_kernel(tc, x, att, Wv, bv, w0, w1, wK, out):
                         quantise_x(x_quantised)
                     if v_quantised is not None and v_quantised % 2 == 1:
                         quantise_v(v_quantised)
-                    if ADD_ENG == "V" and added is not None:
-                        add_identity(added)
             for ch in PE_ORDER:
                 if ch == "t":
                     if turned is not None:

from contextlib import ExitStack

import concourse.mybir as mybir
from concourse.masks import make_identity

F32 = mybir.dt.float32
BF16 = mybir.dt.bfloat16
U32 = mybir.dt.uint32
U8 = mybir.dt.uint8
FP8X4 = mybir.dt.float8_e4m3fn_x4
ALU = mybir.AluOpType
ACT = mybir.ActivationFunctionType

B, N, D, DH = 4, 1024, 512, 128
P = 128
PACK = 4
HALF = 512
ROW_TILES = N // P
UNITS = 4 * B

X_LAG = 0
ATT2_LAG = 3
LIN_LEAD = 1
FILL = 3
FILL_V = 2
LIN_ENG = "GGGS"
PAIR_ENG = "GS"
ADD_ENG = "G"
REG = ["SS", "SS", "SS", "SS"]
ROWBUFS = 2
ACCB = 3
TURNB = 3
SMALLB = 2
MERGE = 1
REGROUP_LATE = 1
X_FIRST = 1
CONST_STEP = 1
W_STEP = 2
EARLY = 1
DRAIN = 1
V_ORDER = "qxg"
PE_ORDER = "tavo"
FLOPS = 2 * B * (N * D * DH + N * N * N + N * N * DH)


def tile_gfsa_pa_t_kernel(tc, x, att, Wv, bv, w0, w1, wK, out):
    nc = tc.nc
    with ExitStack() as ctx:
        const = ctx.enter_context(tc.tile_pool(name="const", bufs=1))
        sbuf = ctx.enter_context(tc.tile_pool(name="sbuf", bufs=3))
        psum_turn = ctx.enter_context(tc.psum_pool(name="psum_turn", bufs=TURNB))
        psum_att2 = ctx.enter_context(tc.psum_pool(name="psum_att2", bufs=ACCB))
        psum_small = ctx.enter_context(tc.psum_pool(name="psum_small", bufs=SMALLB))
        ctx.enter_context(tc.manual_schedule())

        def operand(name, columns, bufs):
            codes = sbuf.tile([P, columns], U32, align_bytes=64, name=name + "_codes", bufs=bufs)
            scales = sbuf.tile([P, columns], U8, align_bytes=64, name=name + "_scales", bufs=bufs)
            return codes, scales

        def columns_of(pair, first, count):
            return pair[0][:, first : first + count], pair[1][:, first : first + count]

        def quantise(pair, grouped):
            nc.vector.quantize_mx(out=pair[0][:].bitcast(FP8X4), scales=pair[1][:], in_=grouped)

        def mx(acc, left, right, start, stop):
            nc.tensor.matmul_mx(
                out=acc,
                lhsT=left[0].bitcast(FP8X4),
                lhsT_scale=left[1],
                rhs=right[0].bitcast(FP8X4),
                rhs_scale=right[1],
                start=start,
                stop=stop,
            )

        a_rows, x_rows = {}, {}
        grouped, codes, xt_grouped, x_q, v_grouped, v_q = {}, {}, {}, {}, {}, {}
        linear, gf_grouped, gf_q = {}, {}, {}
        stores, banks = [], []

        def load_batch(b):
            a_rows[b] = sbuf.tile([P, ROW_TILES, N], BF16, name="a_rows", bufs=ROWBUFS)
            x_rows[b] = sbuf.tile([P, ROW_TILES, D], BF16, name="x_rows", bufs=ROWBUFS)
            a_chunks = att[b, 0].rearrange("(c p e) m -> c p e m", p=P, e=2)
            x_chunks = x[b].rearrange("(c p e) d -> c p e d", p=P, e=2)
            for c in range(ROW_TILES // 2):
                nc.sync.dma_start(out=a_rows[b][:, 2 * c : 2 * c + 2, :], in_=a_chunks[c])
            for c in range(ROW_TILES // 2):
                nc.sync.dma_start(out=x_rows[b][:, 2 * c : 2 * c + 2, :], in_=x_chunks[c])

        load_batch(0)

        ident = const.tile([P, P], F32)
        make_identity(nc, ident[:])

        ident_bf = const.tile([P, P], BF16)
        make_identity(nc, ident_bf[:])

        w0_bf = const.tile([P, 1], BF16)
        w1_bf = const.tile([P, 1], BF16)
        wk_bf = const.tile([P, 1], BF16)
        bias = const.tile([P, DH], BF16)
        wv_rows = const.tile([P, PACK, DH], BF16)
        nc.scalar.dma_start(out=w0_bf[:], in_=w0.partition_broadcast(P))
        nc.scalar.dma_start(out=w1_bf[:], in_=w1.partition_broadcast(P))
        nc.scalar.dma_start(out=wk_bf[:], in_=wK.partition_broadcast(P))
        nc.scalar.dma_start(out=bias[:], in_=bv.partition_broadcast(P))
        nc.scalar.dma_start(
            out=wv_rows[:].rearrange("p (u e) n -> p u e n", e=2),
            in_=Wv.rearrange("(u p e) n -> p u e n", p=P, e=2),
        )
        lin = const.tile([P, 1], F32)
        quad = const.tile([P, 1], F32)
        w0_f32 = const.tile([P, 1], F32)
        w0_ident = const.tile([P, P], F32)
        wv_grouped = const.tile([P, DH, PACK], BF16, align_bytes=64)
        wv_codes = const.tile([P, DH], U32, align_bytes=64)
        wv_scales = const.tile([P, DH], U8, align_bytes=64)

        def prepare_weights():
            nc.vector.tensor_copy(out=wv_grouped[:], in_=wv_rows[:].rearrange("p t n -> p n t"))
            quantise((wv_codes, wv_scales), wv_grouped[:].rearrange("p n t -> p (n t)"))

        def prepare_constants():
            nc.vector.tensor_tensor(out=lin[:], in0=w1_bf[:], in1=wk_bf[:], op=ALU.subtract)
            nc.vector.tensor_scalar(
                out=quad[:], in0=wk_bf[:], scalar1=2.0, scalar2=None, op0=ALU.mult
            )
            nc.vector.tensor_copy(out=w0_f32[:], in_=w0_bf[:])
            nc.vector.tensor_scalar(
                out=w0_ident[:], in0=ident[:], scalar1=w0_f32[:, 0:1], scalar2=None, op0=ALU.mult
            )

        def flat(ap):
            return ap.rearrange("p n t -> p (n t)")

        def turn(words, row_tile, first_word):
            bank = psum_turn.tile([P, 2, 2 * P], F32, name="bank")
            for u in range(2):
                for i in range(2):
                    nc.tensor.transpose(
                        bank[:, u, i * P : (i + 1) * P],
                        words[:, row_tile + i, first_word + u * P : first_word + (u + 1) * P],
                        ident[:],
                    )
            return bank

        def new_grouped(n):
            grouped[n] = sbuf.tile([P, 2 * HALF, PACK], BF16, align_bytes=64, name="grouped", bufs=6)

        def turn_att(n, c):
            b, block = n // 4, n % 4
            bank = turn(a_rows[b][:].bitcast(F32), 2 * block, c * 2 * P)
            out_words = grouped[n][:, c * 2 * P : (c + 1) * 2 * P, :].bitcast(F32)
            nc.scalar.copy(out=out_words, in_=bank[:].rearrange("p u n -> p n u"))

        def turn_x(n):
            b, j = n // 4, n % 4
            bank = turn(x_rows[b][:].bitcast(F32), 2 * j, 0)
            xt_grouped[n] = sbuf.tile([P, 2 * P, PACK], BF16, align_bytes=64, name="xt_grouped")
            nc.scalar.copy(
                out=xt_grouped[n][:].bitcast(F32), in_=bank[:].rearrange("p u n -> p n u")
            )

        def regroup(n, i, engine):
            b, half, g = n // 4, n % 4 // 2, n % 2
            c = 2 * half + i
            lying = a_rows[b][:, PACK * g : PACK * (g + 1), c * 2 * P : (c + 1) * 2 * P]
            lying = lying.rearrange("p t (q e) -> p e q t", e=2)
            dest = grouped[n][:, HALF + i * 2 * P : HALF + (i + 1) * 2 * P, :]
            dest = dest.rearrange("p (e q) t -> p e q t", e=2)
            if engine == "P":
                bank = psum_turn.tile([P, 2, P, PACK], BF16, name="bank")
                for e in range(2):
                    nc.tensor.matmul(
                        out=bank[:, e, :, :], lhsT=ident_bf[:], rhs=lying[:, e, :, :], start=True, stop=True
                    )
                nc.scalar.copy(out=dest, in_=bank[:])
            elif engine == "V":
                nc.vector.tensor_copy(out=dest, in_=lying)
            else:
                nc.scalar.copy(out=dest, in_=lying)

        def quantise_att(n):
            codes[n] = operand("att", 2 * HALF, 9)
            if MERGE:
                quantise(codes[n], flat(grouped[n][:]))
            else:
                for i in range(2):
                    quantise(
                        (codes[n][0][:, i * HALF : (i + 1) * HALF], codes[n][1][:, i * HALF : (i + 1) * HALF]),
                        flat(grouped[n][:, i * HALF : (i + 1) * HALF, :]),
                    )

        def quantise_x(n):
            x_q[n] = operand("x", 2 * P, 4)
            quantise(x_q[n], flat(xt_grouped[n][:]))

        def values(n):
            bank = psum_small.tile([P, PACK, DH], F32, name="small_bank")
            for k in range(PACK):
                mx(
                    bank[:, k, :],
                    columns_of(x_q[n - 1 + k // 2], k % 2 * P, P),
                    (wv_codes[:], wv_scales[:]),
                    True,
                    True,
                )
            v_grouped[n] = sbuf.tile([P, DH, PACK], BF16, align_bytes=64, name="v_grouped", bufs=2)
            nc.vector.tensor_tensor(
                out=v_grouped[n][:],
                in0=bank[:].rearrange("p t d -> p d t"),
                in1=bias[:].unsqueeze(2).to_broadcast([P, DH, PACK]),
                op=ALU.add,
            )

        def quantise_v(n):
            v_q[n] = operand("v", DH, 4)
            quantise(v_q[n], flat(v_grouped[n][:]))

        def att_words(n, k):
            b, side = n // 4, n % 2
            return 4 * b + 2 * side + k // 2, n % 4 // 2

        def linear_part(n, who):
            b, g, side = n // 4, n % 4 // 2, n % 2
            if side == g:
                if "S" in who:
                    linear[n] = sbuf.tile([P, 2, P, PACK, 2], F32, align_bytes=64, name="linear_or_gf", bufs=3)
                for u in range(2):
                    if PAIR_ENG[u] not in who:
                        continue
                    source = grouped[4 * b + 2 * side + u][:, g * 2 * P : (g + 1) * 2 * P, :]
                    scale_by(PAIR_ENG[u], linear[n][:, u], source.rearrange("p (h q) t -> p q t h", h=2))
                if "G" in who:
                    add_identity(n)
            else:
                linear[n] = sbuf.tile([P, PACK, P, PACK], F32, align_bytes=64, name="linear_or_gf", bufs=3)
                for k in range(PACK):
                    u = 4 * b + 2 * side + k // 2
                    first = g * 2 * P + k % 2 * P
                    scale_by(LIN_ENG[k], linear[n][:, k, :, :], grouped[u][:, first : first + P, :])

        def scale_by(engine, dest, src):
            if engine == "G":
                nc.gpsimd.tensor_scalar(out=dest, in0=src, scalar1=lin[:, 0:1], scalar2=0.0, op0=ALU.mult, op1=ALU.add)
            elif engine == "V":
                nc.vector.tensor_scalar(out=dest, in0=src, scalar1=lin[:, 0:1], scalar2=None, op0=ALU.mult)
            else:
                nc.scalar.activation(out=dest, in_=src, func=ACT.Copy, scale=lin[:, 0:1])

        def add_identity(n):
            for u in range(2):
                pair = linear[n][:, u].rearrange("p q t h -> p q (t h)")
                blocks = pair[:, :, PACK * u : PACK * u + PACK : 3]
                nc.gpsimd.tensor_tensor(
                    out=blocks, in0=blocks, in1=w0_ident[:].unsqueeze(2).to_broadcast([P, P, 2]), op=ALU.add)

        def att2(n, k):
            b, g, side = n // 4, n % 4 // 2, n % 2
            acc = psum_att2.tile([P, PACK, P], F32, name="acc")
            for t in range(PACK):
                for c in range(2):
                    mx(
                        acc[:, t, :],
                        columns_of(codes[4 * b + 2 * g + c], HALF + t * P, P),
                        columns_of(codes[4 * b + 2 * side + k // 2], c * 2 * P + k % 2 * P, P),
                        c == 0,
                        c == 1,
                    )
            if side == g:
                part = linear[n][:, k // 2, :, :, k % 2]
            else:
                part = linear[n][:, k, :, :]
            nc.vector.scalar_tensor_tensor(
                out=gf_grouped[n][:, k * P : (k + 1) * P, :],
                in0=acc[:].rearrange("p t n -> p n t"),
                scalar=quad[:, 0:1],
                in1=part,
                op0=ALU.mult,
                op1=ALU.add,
            )

        def quantise_gf(n):
            gf_q[n] = operand("gf", HALF, 4)
            quantise(gf_q[n], flat(gf_grouped[n][:]))

        def output(n):
            b, side = n // 4, n % 2
            bank = psum_small.tile([P, PACK, DH], F32, name="small_bank")
            for k in range(PACK):
                for c in range(2):
                    mx(
                        bank[:, k, :],
                        columns_of(gf_q[n - 2 + 2 * c], k * P, P),
                        columns_of(v_q[4 * b + 2 * c + 1], 0, DH),
                        c == 0,
                        c == 1,
                    )
            banks.append((b, side, bank))

        def drain():
            b, side, bank = banks.pop()
            o_rows = sbuf.tile([P, PACK, DH], F32, name="o_rows", bufs=2)
            nc.scalar.copy(out=o_rows[:], in_=bank[:])
            stores.append((b, side, o_rows))

        def store():
            b, side, o_rows = stores.pop()
            nc.scalar.dma_start(
                out=out[b, side * HALF : (side + 1) * HALF, :].rearrange("(u p e) d -> p u e d", p=P, e=2),
                in_=o_rows[:].rearrange("p (u e) d -> p u e d", e=2),
            )

        def unit(step, lag):
            return step - lag if 0 <= step - lag < UNITS else None

        for step in range(UNITS + ATT2_LAG + 2):
            turned = unit(step, 0)
            quantised = unit(step, 1)
            x_turned = unit(step, X_LAG)
            x_quantised = unit(step, X_LAG + 1)
            valued = unit(step, X_LAG + 2)
            v_quantised = unit(step, X_LAG + 3)
            lined = unit(step, ATT2_LAG - LIN_LEAD)
            added = unit(step, ATT2_LAG)
            squared = unit(step, ATT2_LAG)
            completed = unit(step, ATT2_LAG + 1)
            if turned is not None and turned % 4 == 0 and turned // 4 + 1 < B:
                load_batch(turned // 4 + 1)
            if step == CONST_STEP:
                prepare_constants()
            if step == W_STEP:
                prepare_weights()
            if squared is not None:
                gf_grouped[squared] = sbuf.tile([P, HALF, PACK], BF16, align_bytes=64, name="linear_or_gf", bufs=3)
            if DRAIN == 0 and banks:
                drain()
            if EARLY and lined is not None and lined % 2 == lined % 4 // 2:
                linear_part(lined, "S")
            if REGROUP_LATE and step < FILL and quantised is not None:
                quantise_att(quantised)
                quantised = None
            if turned is not None:
                new_grouped(turned)
                ways = REG[turned % 4]
                if step < FILL:
                    ways = ("V" * FILL_V + ways)[:2]
                for i in range(2):
                    if ways[i] != "P":
                        regroup(turned, i, ways[i])
            if DRAIN == 1 and banks:
                drain()
            for ch in V_ORDER:
                if ch == "g" and completed is not None:
                    quantise_gf(completed)
                if ch == "q" and quantised is not None:
                    quantise_att(quantised)
                if ch == "x":
                    if x_quantised is not None and step > X_FIRST:
                        if step == X_FIRST + 1:
                            for j in range(X_FIRST):
                                quantise_x(j)
                        quantise_x(x_quantised)
                    if v_quantised is not None and v_quantised % 2 == 1:
                        quantise_v(v_quantised)
            for ch in PE_ORDER:
                if ch == "t":
                    if turned is not None:
                        turn_att(turned, 0)
                        turn_att(turned, 1)
                        for i in range(2):
                            if ways[i] == "P":
                                regroup(turned, i, "P")
                    if x_turned is not None and step >= X_FIRST:
                        if step == X_FIRST:
                            for j in range(X_FIRST):
                                turn_x(j)
                        turn_x(x_turned)
                if ch == "a" and squared is not None:
                    for k in range(PACK):
                        att2(squared, k)
                if ch == "v" and valued is not None and valued % 2 == 1:
                    values(valued)
                if ch == "o" and completed is not None and completed % 4 >= 2:
                    output(completed)
            if stores:
                store()
            if lined is not None:
                linear_part(lined, "G" if EARLY and lined % 2 == lined % 4 // 2 else "SG")
